import numpy as np
import ml_dtypes


def mxq(x, axis, fmt="e4m3"):
    dtype, down = {"e4m3": (ml_dtypes.float8_e4m3fn, 7), "e5m2": (ml_dtypes.float8_e5m2, 14)}[fmt]
    v = np.moveaxis(np.asarray(x, np.float32).astype(ml_dtypes.bfloat16).astype(np.float64), axis, -1)
    blocks = v.reshape(v.shape[:-1] + (-1, 32))
    amax = np.abs(blocks).max(-1, keepdims=True)
    byte = np.maximum(np.where(amax > 0, np.frexp(amax)[1] - 1 + 127, 0) - down, 1)
    scale = np.exp2(byte - 127.0)
    codes = (blocks / scale).astype(np.float32).astype(dtype).astype(np.float64)
    return np.moveaxis((codes * scale).reshape(v.shape), -1, axis)


WIDE = False


def mx_kscale(k):
    if not WIDE:
        return np.ones(k)
    levels = np.array([10, -10, 5, -5, 0])
    a = np.random.permutation(np.resize(levels, k // 512 * 4)).reshape(k // 512, 4)
    idx = np.arange(k)
    return np.exp2(a[idx // 512, idx % 128 // 32])


BF16 = ml_dtypes.bfloat16


def bf(x):
    return np.asarray(x, np.float32).astype(BF16)


def f64(x):
    return np.asarray(x).astype(np.float64)


B, T, V, C, K, R = 4, 8, 32, 512, 1024, 256


def setup_inputs():
    n = np.random.standard_normal
    s = mx_kscale(C)
    x = 0.7 * n((B, 1, V, C)) + 0.7 * n((B, T, V, C))
    return {
        "x": bf(x * s),
        "A": bf(np.eye(V) + 0.1 * n((K, V, V))),
        "lam": bf(0.25 + 0.1 * np.random.random(1)),
        "phi_w": bf(n((C, K)) / np.sqrt(C) / s[:, None]),
        "phi_b": bf(0.3 * n(K)),
        "theta_w": bf(n((C, K)) / np.sqrt(C) / s[:, None]),
        "theta_b": bf(0.3 * n(K)),
        "kappa_w": bf(n((K, K)) / np.sqrt(K)),
        "kappa_b": bf(0.3 * n(K)),
    }


def reference(x, A, lam, phi_w, phi_b, theta_w, theta_b, kappa_w, kappa_b):
    xq = mxq(f64(x), 3, "e4m3")
    phi_x = ((xq @ mxq(f64(phi_w), 0, "e4m3")) + f64(phi_b)).mean(axis=1)
    theta_x = ((xq @ mxq(f64(theta_w), 0, "e4m3")) + f64(theta_b)).mean(axis=1)
    F_ij = np.tanh(phi_x[:, :, None, :] - theta_x[:, None, :, :])
    A_hat = np.transpose((mxq(F_ij, 3, "e4m3") @ mxq(f64(kappa_w), 0, "e4m3")) + f64(kappa_b), (0, 3, 1, 2))
    return f64(A)[None] + f64(lam) * A_hat

@@ -1,0 +1,271 @@
+from contextlib import ExitStack
+
+import concourse.mybir as mybir
+from concourse.masks import make_identity
+
+F32 = mybir.dt.float32
+BF16 = mybir.dt.bfloat16
+U32 = mybir.dt.uint32
+U8 = mybir.dt.uint8
+FP8X4 = mybir.dt.float8_e4m3fn_x4
+ALU = mybir.AluOpType
+ACT = mybir.ActivationFunctionType
+
+P = 128
+PACK = 4
+B, T, V, C, K = 4, 8, 32, 512, 1024
+ROWS = B * V
+X_TILES = B * T * V // P
+PASSES = K // (P * PACK)
+K_TILES = K // P
+N_TILE = 512
+U_CHUNK = N_TILE // V
+U_CHUNKS = V // U_CHUNK
+RUN = 4
+LAG = 2
+
+FLOPS = 2 * (B * T * V) * C * K * 2 + 2 * (B * V * V) * K * K
+
+
+def quantise_columns(nc, copy, grouped_pool, rows, codes, scales):
+    grouped = grouped_pool.tile([P, N_TILE * PACK], BF16, name="grouped", align_bytes=64)
+    copy(
+        out=grouped[:].rearrange("p (c i s) -> p c s i", i=RUN, s=PACK),
+        in_=rows.rearrange("p s (c i) -> p c s i", i=RUN),
+    )
+    nc.vector.quantize_mx(out=codes.bitcast(FP8X4), scales=scales, in_=grouped[:])
+
+
+def tile_attgcn_pa_kernel(
+    tc, x, A, lam, phi_w, phi_b, theta_w, theta_b, kappa_w, kappa_b, out
+):
+    nc = tc.nc
+    with ExitStack() as pools:
+        const = pools.enter_context(tc.tile_pool(name="const", bufs=1))
+        raw_pool = pools.enter_context(tc.tile_pool(name="raw", bufs=4))
+        grouped_pool = pools.enter_context(tc.tile_pool(name="grouped", bufs=3))
+        diff_pool = pools.enter_context(tc.tile_pool(name="diff", bufs=4))
+        f_pool = pools.enter_context(tc.tile_pool(name="f", bufs=4))
+        f_mx_pool = pools.enter_context(tc.tile_pool(name="f_mx", bufs=8))
+        result_pool = pools.enter_context(tc.tile_pool(name="result", bufs=6))
+        psum_keep = pools.enter_context(tc.psum_pool(name="psum_keep", bufs=1))
+        psum_work = pools.enter_context(tc.psum_pool(name="psum_work", bufs=6))
+
+        bias_rows = const.tile([P, P], BF16, name="bias_rows")
+        nc.vector.memset(bias_rows[:], 0.0)
+        for i, bias in enumerate((phi_b, theta_b, kappa_b)):
+            nc.scalar.dma_start(
+                out=bias_rows[i * K_TILES : (i + 1) * K_TILES, :],
+                in_=bias.rearrange("(r q) -> r q", q=P),
+            )
+        lam_bf = const.tile([P, 1], BF16, name="lam_bf")
+        nc.scalar.dma_start(out=lam_bf[:], in_=lam.partition_broadcast(P))
+
+        def raw_tile(name):
+            return raw_pool.tile([P, PACK * K], BF16, name=name, tag="raw")
+
+        x_raw = raw_tile("x_raw")
+        x_rows = x_raw[:].rearrange("p (n c) -> p n c", c=C)
+        x_view = x.flatten_outer_dims().rearrange("(n p) c -> p n c", p=P)
+        for half in range(2):
+            tiles = slice(half * X_TILES // 2, (half + 1) * X_TILES // 2)
+            nc.sync.dma_start(out=x_rows[:, tiles, :], in_=x_view[:, tiles, :])
+
+        w_raw = {"phi": raw_tile("phi_raw"), "theta": raw_tile("theta_raw")}
+        w_dram = {"phi": phi_w, "theta": theta_w}
+        for g in range(PASSES):
+            cols = slice(g * N_TILE, (g + 1) * N_TILE)
+            for name in ("phi", "theta"):
+                for h in range(2):
+                    nc.sync.dma_start(
+                        out=w_raw[name][:].rearrange("q (h e n) -> q h e n", h=2, e=2)[:, h, :, cols],
+                        in_=w_dram[name].rearrange("(h q e) n -> q h e n", h=2, e=2)[:, h, :, cols],
+                    )
+
+        def load_four_rows(name, view):
+            raw = raw_tile(name)
+            nc.sync.dma_start(out=raw[:].rearrange("q (s n) -> q s n", s=PACK), in_=view)
+            return raw
+
+        kappa_view = kappa_w.rearrange("(a q) n -> q a n", q=P)
+        kappa_raw = [
+            load_four_rows("kappa_raw%d" % g, kappa_view[:, g * PACK : (g + 1) * PACK, :])
+            for g in range(PASSES)
+        ]
+        a_view = A.rearrange("(a q) u v -> q a (u v)", q=P)
+        a_raw = [
+            load_four_rows("a_raw%d" % half, a_view[:, half * PACK : (half + 1) * PACK, :])
+            for half in range(K_TILES // PACK)
+        ]
+
+        ident = const.tile([P, P], F32, name="ident")
+        make_identity(nc, ident[:])
+
+        x_words = x_raw[:].bitcast(F32)
+        x_grouped = const.tile([P, T * ROWS * PACK], BF16, name="x_grouped", align_bytes=64)
+        x_grouped_words = x_grouped[:].bitcast(F32).rearrange(
+            "q (t b v h) -> q t b v h", t=T, b=B, v=V
+        )
+        words = C // 2
+        for b in range(B):
+            x_t = psum_work.tile([P, 2, 2 * P], F32, name="x_t", tag="work")
+            for h in range(2):
+                for th in range(2):
+                    first = (2 * b + th) * words + h * P
+                    nc.tensor.transpose(
+                        x_t[:, h, th * P : (th + 1) * P], x_words[:, first : first + P], ident[:]
+                    )
+            copy = nc.vector.tensor_copy if b % 2 == 0 else nc.scalar.copy
+            copy(
+                out=x_grouped_words[:, :, b, :, :],
+                in_=x_t[:].rearrange("q h (t v) -> q t v h", v=V),
+            )
+        x_codes = const.tile([P, T * ROWS], U32, name="x_codes", align_bytes=64)
+        x_scales = const.tile([P, T * ROWS], U8, name="x_scales", align_bytes=64)
+        nc.vector.quantize_mx(out=x_codes[:].bitcast(FP8X4), scales=x_scales[:], in_=x_grouped[:])
+
+        bias_rows_f32 = const.tile([P, P], F32, name="bias_rows_f32")
+        nc.vector.tensor_copy(out=bias_rows_f32[:], in_=bias_rows[:])
+        bias_ps = psum_work.tile([P, N_TILE], F32, name="bias_ps", tag="work")
+        nc.tensor.transpose(bias_ps[:, 0:P], bias_rows_f32[:], ident[:])
+        bias_cols = const.tile([P, 3 * K_TILES], F32, name="bias_cols")
+        nc.vector.tensor_copy(out=bias_cols[:], in_=bias_ps[:, 0 : 3 * K_TILES])
+        phi_b_cols = bias_cols[:, 0:K_TILES]
+        theta_b_cols = bias_cols[:, K_TILES : 2 * K_TILES]
+        kappa_b_cols = bias_cols[:, 2 * K_TILES : 3 * K_TILES]
+
+        bias_diff = const.tile([P, K_TILES], F32, name="bias_diff")
+        nc.vector.tensor_sub(out=bias_diff[:], in0=theta_b_cols, in1=phi_b_cols)
+        bias_diff_t = const.tile([P, K_TILES], F32, name="bias_diff_t")
+        nc.vector.tensor_scalar_mul(out=bias_diff_t[:], in0=bias_diff[:], scalar1=float(T))
+        lam_col = const.tile([P, 1], F32, name="lam_col")
+        nc.vector.tensor_copy(out=lam_col[:], in_=lam_bf[:])
+        lam_kappa_b = const.tile([P, K_TILES], F32, name="lam_kappa_b")
+        nc.vector.tensor_scalar_mul(out=lam_kappa_b[:], in0=kappa_b_cols, scalar1=lam_col[:, 0:1])
+
+        w_codes = {}
+        w_scales = {}
+        for name in ("phi", "theta"):
+            w_codes[name] = const.tile([P, K], U32, name=name + "_codes", align_bytes=64)
+            w_scales[name] = const.tile([P, K], U8, name=name + "_scales", align_bytes=64)
+        w_rows = {name: w_raw[name][:].rearrange("q (s n) -> q s n", s=PACK) for name in w_raw}
+        w_copy = {"phi": nc.vector.tensor_copy, "theta": nc.scalar.copy}
+        th_t = const.tile([P, PASSES, ROWS, PACK], F32, name="th_t")
+        sum_p = []
+        for g in range(PASSES):
+            cols = slice(g * N_TILE, (g + 1) * N_TILE)
+            sums = {
+                "phi": psum_keep.tile([P, PACK, ROWS], F32, name="sum_p%d" % g),
+                "theta": psum_work.tile([P, PACK, ROWS], F32, name="sum_th", tag="work"),
+            }
+            for name in ("phi", "theta"):
+                quantise_columns(
+                    nc, w_copy[name], grouped_pool, w_rows[name][:, :, cols],
+                    w_codes[name][:, cols], w_scales[name][:, cols],
+                )
+                for j in range(PACK):
+                    tile_cols = slice((g * PACK + j) * P, (g * PACK + j + 1) * P)
+                    for t in range(T):
+                        step_cols = slice(t * ROWS, (t + 1) * ROWS)
+                        nc.tensor.matmul_mx(
+                            out=sums[name][:, j, :],
+                            lhsT=w_codes[name][:, tile_cols].bitcast(FP8X4),
+                            lhsT_scale=w_scales[name][:, tile_cols],
+                            rhs=x_codes[:, step_cols].bitcast(FP8X4),
+                            rhs_scale=x_scales[:, step_cols],
+                            start=(t == 0),
+                            stop=(t == T - 1),
+                        )
+            sum_p.append(sums["phi"])
+            nc.vector.tensor_tensor(
+                out=th_t[:, g, :, :],
+                in0=sums["theta"][:].rearrange("q j r -> q r j"),
+                in1=bias_diff_t[:, g * PACK : (g + 1) * PACK].unsqueeze(1).to_broadcast(
+                    [P, ROWS, PACK]
+                ),
+                op=ALU.add,
+            )
+
+        kappa_codes = const.tile([P, PASSES, K], U32, name="kappa_codes", align_bytes=64)
+        kappa_scales = const.tile([P, PASSES, K], U8, name="kappa_scales", align_bytes=64)
+        for g in range(PASSES):
+            rows = kappa_raw[g][:].rearrange("q (s n) -> q s n", s=PACK)
+            for half in range(K // N_TILE):
+                cols = slice(half * N_TILE, (half + 1) * N_TILE)
+                quantise_columns(
+                    nc, nc.scalar.copy, grouped_pool, rows[:, :, cols],
+                    kappa_codes[:, g, cols], kappa_scales[:, g, cols],
+                )
+        a_plus = const.tile([P, K_TILES, V * V], F32, name="a_plus")
+        for kt in range(K_TILES):
+            nc.scalar.activation(
+                out=a_plus[:, kt, :],
+                in_=a_raw[kt // PACK][:, (kt % PACK) * V * V : (kt % PACK + 1) * V * V],
+                func=ACT.Identity,
+                bias=lam_kappa_b[:, kt : kt + 1],
+            )
+
+        f_codes = {}
+        f_scales = {}
+        f_bf16 = {}
+
+        def subtract_and_tanh(b, g, uc):
+            first_u = b * V + uc * U_CHUNK
+            shape = [P, U_CHUNK, V, PACK]
+            diff = diff_pool.tile(shape, F32, name="diff")
+            nc.vector.tensor_tensor(
+                out=diff[:],
+                in0=sum_p[g][:, :, first_u : first_u + U_CHUNK]
+                .rearrange("q j u -> q u j").unsqueeze(2).to_broadcast(shape),
+                in1=th_t[:, g, b * V : (b + 1) * V, :].unsqueeze(1).to_broadcast(shape),
+                op=ALU.subtract,
+            )
+            f = f_pool.tile([P, N_TILE * PACK], BF16, name="f", align_bytes=64)
+            nc.scalar.activation(
+                out=f[:], in_=diff[:].rearrange("q u v j -> q (u v j)"), func=ACT.Tanh,
+                scale=1.0 / T,
+            )
+            f_bf16[(b, g, uc)] = f
+
+        def quantise_f(b, g, uc):
+            codes = f_mx_pool.tile([P, N_TILE], U32, name="f_codes", align_bytes=64)
+            scales = f_mx_pool.tile([P, N_TILE], U8, name="f_scales", align_bytes=64)
+            nc.vector.quantize_mx(
+                out=codes[:].bitcast(FP8X4), scales=scales[:], in_=f_bf16[(b, g, uc)][:]
+            )
+            f_codes[(b, g, uc)] = codes
+            f_scales[(b, g, uc)] = scales
+
+        def multiply_and_store(b, uc):
+            cols = slice(uc * N_TILE, (uc + 1) * N_TILE)
+            out_view = out[b].rearrange("(a q) u v -> q a (u v)", q=P)
+            for kt in range(K_TILES):
+                tile_cols = slice(kt * P, (kt + 1) * P)
+                acc = psum_work.tile([P, N_TILE], F32, name="acc", tag="work")
+                for g in range(PASSES):
+                    nc.tensor.matmul_mx(
+                        out=acc[:],
+                        lhsT=kappa_codes[:, g, tile_cols].bitcast(FP8X4),
+                        lhsT_scale=kappa_scales[:, g, tile_cols],
+                        rhs=f_codes[(b, g, uc)][:].bitcast(FP8X4),
+                        rhs_scale=f_scales[(b, g, uc)][:],
+                        start=(g == 0),
+                        stop=(g == PASSES - 1),
+                    )
+                result = result_pool.tile([P, N_TILE], F32, name="result")
+                nc.vector.scalar_tensor_tensor(
+                    out=result[:], in0=acc[:], scalar=lam_col[:, 0:1], in1=a_plus[:, kt, cols],
+                    op0=ALU.mult, op1=ALU.add,
+                )
+                nc.sync.dma_start(out=out_view[:, kt, cols], in_=result[:])
+
+        chunks = [(b, g, uc) for b in range(B) for g in range(PASSES) for uc in range(U_CHUNKS)]
+        for step in range(len(chunks) + LAG + 1):
+            if step < len(chunks):
+                subtract_and_tanh(*chunks[step])
+            if 0 <= step - LAG < len(chunks):
+                quantise_f(*chunks[step - LAG])
+            if 0 <= step - LAG - 1 < len(chunks):
+                b, g, uc = chunks[step - LAG - 1]
+                if g == PASSES - 1:
+                    multiply_and_store(b, uc)

@@ -23,6 +23,8 @@ U_CHUNK = N_TILE // V
 U_CHUNKS = V // U_CHUNK
 RUN = 4
 LAG = 2
+U_GPSIMD = 12
+U_VECTOR = U_CHUNK - U_GPSIMD
 
 FLOPS = 2 * (B * T * V) * C * K * 2 + 2 * (B * V * V) * K * K
 
@@ -151,6 +153,7 @@ def tile_attgcn_pa_kernel(
         w_rows = {name: w_raw[name][:].rearrange("q (s n) -> q s n", s=PACK) for name in w_raw}
         w_copy = {"phi": nc.vector.tensor_copy, "theta": nc.scalar.copy}
         th_t = const.tile([P, PASSES, ROWS, PACK], F32, name="th_t")
+        p_t = const.tile([P, PASSES, ROWS, PACK], F32, name="p_t")
         sum_p = []
         for g in range(PASSES):
             cols = slice(g * N_TILE, (g + 1) * N_TILE)
@@ -177,6 +180,7 @@ def tile_attgcn_pa_kernel(
                             stop=(t == T - 1),
                         )
             sum_p.append(sums["phi"])
+            nc.vector.tensor_copy(out=p_t[:, g, :, :], in_=sums["phi"][:].rearrange("q j r -> q r j"))
             nc.vector.tensor_tensor(
                 out=th_t[:, g, :, :],
                 in0=sums["theta"][:].rearrange("q j r -> q r j"),
@@ -211,13 +215,21 @@ def tile_attgcn_pa_kernel(
 
         def subtract_and_tanh(b, g, uc):
             first_u = b * V + uc * U_CHUNK
-            shape = [P, U_CHUNK, V, PACK]
-            diff = diff_pool.tile(shape, F32, name="diff")
+            split_u = first_u + U_VECTOR
+            th_rows = th_t[:, g, b * V : (b + 1) * V, :].unsqueeze(1)
+            diff = diff_pool.tile([P, U_CHUNK, V, PACK], F32, name="diff")
             nc.vector.tensor_tensor(
-                out=diff[:],
-                in0=sum_p[g][:, :, first_u : first_u + U_CHUNK]
-                .rearrange("q j u -> q u j").unsqueeze(2).to_broadcast(shape),
-                in1=th_t[:, g, b * V : (b + 1) * V, :].unsqueeze(1).to_broadcast(shape),
+                out=diff[:, 0:U_VECTOR, :, :],
+                in0=sum_p[g][:, :, first_u:split_u]
+                .rearrange("q j u -> q u j").unsqueeze(2).to_broadcast([P, U_VECTOR, V, PACK]),
+                in1=th_rows.to_broadcast([P, U_VECTOR, V, PACK]),
+                op=ALU.subtract,
+            )
+            nc.gpsimd.tensor_tensor(
+                out=diff[:, U_VECTOR:U_CHUNK, :, :],
+                in0=p_t[:, g, split_u : first_u + U_CHUNK, :]
+                .unsqueeze(2).to_broadcast([P, U_GPSIMD, V, PACK]),
+                in1=th_rows.to_broadcast([P, U_GPSIMD, V, PACK]),
                 op=ALU.subtract,
             )
             f = f_pool.tile([P, N_TILE * PACK], BF16, name="f", align_bytes=64)

@@ -23,7 +23,7 @@ U_CHUNK = N_TILE // V
 U_CHUNKS = V // U_CHUNK
 RUN = 4
 LAG = 2
-U_GPSIMD = 12
+U_GPSIMD = 8
 U_VECTOR = U_CHUNK - U_GPSIMD
 
 FLOPS = 2 * (B * T * V) * C * K * 2 + 2 * (B * V * V) * K * K

@@ -23,8 +23,10 @@ U_CHUNK = N_TILE // V
 U_CHUNKS = V // U_CHUNK
 RUN = 4
 LAG = 2
-U_GPSIMD = 8
-U_VECTOR = U_CHUNK - U_GPSIMD
+U_GPSIMD = 5
+U_SCALAR = 3
+U_VECTOR = U_CHUNK - U_GPSIMD - U_SCALAR
+U_DIFF = U_VECTOR + U_GPSIMD
 
 FLOPS = 2 * (B * T * V) * C * K * 2 + 2 * (B * V * V) * K * K
 
@@ -154,6 +156,7 @@ def tile_attgcn_pa_kernel(
         w_copy = {"phi": nc.vector.tensor_copy, "theta": nc.scalar.copy}
         th_t = const.tile([P, PASSES, ROWS, PACK], F32, name="th_t")
         p_t = const.tile([P, PASSES, ROWS, PACK], F32, name="p_t")
+        p_mean = const.tile([P, PASSES, ROWS, PACK], F32, name="p_mean")
         sum_p = []
         for g in range(PASSES):
             cols = slice(g * N_TILE, (g + 1) * N_TILE)
@@ -181,6 +184,7 @@ def tile_attgcn_pa_kernel(
                         )
             sum_p.append(sums["phi"])
             nc.vector.tensor_copy(out=p_t[:, g, :, :], in_=sums["phi"][:].rearrange("q j r -> q r j"))
+            nc.scalar.mul(out=p_mean[:, g, :, :], in_=p_t[:, g, :, :], mul=1.0 / T)
             nc.vector.tensor_tensor(
                 out=th_t[:, g, :, :],
                 in0=sums["theta"][:].rearrange("q j r -> q r j"),
@@ -216,27 +220,34 @@ def tile_attgcn_pa_kernel(
         def subtract_and_tanh(b, g, uc):
             first_u = b * V + uc * U_CHUNK
             split_u = first_u + U_VECTOR
-            th_rows = th_t[:, g, b * V : (b + 1) * V, :].unsqueeze(1)
-            diff = diff_pool.tile([P, U_CHUNK, V, PACK], F32, name="diff")
+            th_rows = th_t[:, g, b * V : (b + 1) * V, :]
+            diff = diff_pool.tile([P, U_DIFF, V, PACK], F32, name="diff")
             nc.vector.tensor_tensor(
                 out=diff[:, 0:U_VECTOR, :, :],
                 in0=sum_p[g][:, :, first_u:split_u]
                 .rearrange("q j u -> q u j").unsqueeze(2).to_broadcast([P, U_VECTOR, V, PACK]),
-                in1=th_rows.to_broadcast([P, U_VECTOR, V, PACK]),
+                in1=th_rows.unsqueeze(1).to_broadcast([P, U_VECTOR, V, PACK]),
                 op=ALU.subtract,
             )
             nc.gpsimd.tensor_tensor(
-                out=diff[:, U_VECTOR:U_CHUNK, :, :],
-                in0=p_t[:, g, split_u : first_u + U_CHUNK, :]
+                out=diff[:, U_VECTOR:U_DIFF, :, :],
+                in0=p_t[:, g, split_u : first_u + U_DIFF, :]
                 .unsqueeze(2).to_broadcast([P, U_GPSIMD, V, PACK]),
-                in1=th_rows.to_broadcast([P, U_GPSIMD, V, PACK]),
+                in1=th_rows.unsqueeze(1).to_broadcast([P, U_GPSIMD, V, PACK]),
                 op=ALU.subtract,
             )
             f = f_pool.tile([P, N_TILE * PACK], BF16, name="f", align_bytes=64)
             nc.scalar.activation(
-                out=f[:], in_=diff[:].rearrange("q u v j -> q (u v j)"), func=ACT.Tanh,
-                scale=1.0 / T,
+                out=f[:, 0 : U_DIFF * V * PACK], in_=diff[:].rearrange("q u v j -> q (u v j)"),
+                func=ACT.Tanh, scale=1.0 / T,
             )
+            f_rows = f[:].rearrange("q (u v j) -> q u v j", v=V, j=PACK)
+            for u in range(U_DIFF, U_CHUNK):
+                for j in range(PACK):
+                    nc.scalar.activation(
+                        out=f_rows[:, u, :, j], in_=th_rows[:, :, j], func=ACT.Tanh,
+                        scale=-1.0 / T, bias=p_mean[:, g, first_u + u, j : j + 1],
+                    )
             f_bf16[(b, g, uc)] = f
 
         def quantise_f(b, g, uc):

@@ -31,29 +31,30 @@ U_DIFF = U_VECTOR + U_GPSIMD
 FLOPS = 2 * (B * T * V) * C * K * 2 + 2 * (B * V * V) * K * K
 
 
-def quantise_columns(nc, copy, grouped_pool, rows, codes, scales):
+def regroup_columns(copy, grouped_pool, rows):
     grouped = grouped_pool.tile([P, N_TILE * PACK], BF16, name="grouped", align_bytes=64)
     copy(
         out=grouped[:].rearrange("p (c i s) -> p c s i", i=RUN, s=PACK),
         in_=rows.rearrange("p s (c i) -> p c s i", i=RUN),
     )
-    nc.vector.quantize_mx(out=codes.bitcast(FP8X4), scales=scales, in_=grouped[:])
+    return grouped
 
 
 def tile_attgcn_pa_kernel(
     tc, x, A, lam, phi_w, phi_b, theta_w, theta_b, kappa_w, kappa_b, out
 ):
     nc = tc.nc
-    with ExitStack() as pools:
-        const = pools.enter_context(tc.tile_pool(name="const", bufs=1))
-        raw_pool = pools.enter_context(tc.tile_pool(name="raw", bufs=4))
-        grouped_pool = pools.enter_context(tc.tile_pool(name="grouped", bufs=3))
-        diff_pool = pools.enter_context(tc.tile_pool(name="diff", bufs=4))
-        f_pool = pools.enter_context(tc.tile_pool(name="f", bufs=4))
-        f_mx_pool = pools.enter_context(tc.tile_pool(name="f_mx", bufs=8))
-        result_pool = pools.enter_context(tc.tile_pool(name="result", bufs=6))
-        psum_keep = pools.enter_context(tc.psum_pool(name="psum_keep", bufs=1))
-        psum_work = pools.enter_context(tc.psum_pool(name="psum_work", bufs=6))
+    with ExitStack() as stack:
+        const = stack.enter_context(tc.tile_pool(name="const", bufs=1))
+        raw_pool = stack.enter_context(tc.tile_pool(name="raw", bufs=5))
+        grouped_pool = stack.enter_context(tc.tile_pool(name="grouped", bufs=3))
+        diff_pool = stack.enter_context(tc.tile_pool(name="diff", bufs=4))
+        f_pool = stack.enter_context(tc.tile_pool(name="f", bufs=4))
+        f_mx_pool = stack.enter_context(tc.tile_pool(name="f_mx", bufs=8))
+        result_pool = stack.enter_context(tc.tile_pool(name="result", bufs=6))
+        psum_keep = stack.enter_context(tc.psum_pool(name="psum_keep", bufs=1))
+        psum_work = stack.enter_context(tc.psum_pool(name="psum_work", bufs=6))
+        stack.enter_context(tc.manual_schedule())
 
         bias_rows = const.tile([P, P], BF16, name="bias_rows")
         nc.vector.memset(bias_rows[:], 0.0)
@@ -91,19 +92,22 @@ def tile_attgcn_pa_kernel(
             nc.sync.dma_start(out=raw[:].rearrange("q (s n) -> q s n", s=PACK), in_=view)
             return raw
 
-        kappa_view = kappa_w.rearrange("(a q) n -> q a n", q=P)
-        kappa_raw = [
-            load_four_rows("kappa_raw%d" % g, kappa_view[:, g * PACK : (g + 1) * PACK, :])
-            for g in range(PASSES)
-        ]
         a_view = A.rearrange("(a q) u v -> q a (u v)", q=P)
         a_raw = [
             load_four_rows("a_raw%d" % half, a_view[:, half * PACK : (half + 1) * PACK, :])
             for half in range(K_TILES // PACK)
         ]
+        kappa_view = kappa_w.rearrange("(a q) n -> q a n", q=P)
+        kappa_raw = [
+            load_four_rows("kappa_raw%d" % g, kappa_view[:, g * PACK : (g + 1) * PACK, :])
+            for g in range(PASSES)
+        ]
 
         ident = const.tile([P, P], F32, name="ident")
         make_identity(nc, ident[:])
+
+        bias_rows_f32 = const.tile([P, P], F32, name="bias_rows_f32")
+        nc.vector.tensor_copy(out=bias_rows_f32[:], in_=bias_rows[:])
 
         x_words = x_raw[:].bitcast(F32)
         x_grouped = const.tile([P, T * ROWS * PACK], BF16, name="x_grouped", align_bytes=64)
@@ -124,14 +128,13 @@ def tile_attgcn_pa_kernel(
                 out=x_grouped_words[:, :, b, :, :],
                 in_=x_t[:].rearrange("q h (t v) -> q t v h", v=V),
             )
+        bias_ps = psum_work.tile([P, N_TILE], F32, name="bias_ps", tag="work")
+        nc.tensor.transpose(bias_ps[:, 0:P], bias_rows_f32[:], ident[:])
+
         x_codes = const.tile([P, T * ROWS], U32, name="x_codes", align_bytes=64)
         x_scales = const.tile([P, T * ROWS], U8, name="x_scales", align_bytes=64)
         nc.vector.quantize_mx(out=x_codes[:].bitcast(FP8X4), scales=x_scales[:], in_=x_grouped[:])
 
-        bias_rows_f32 = const.tile([P, P], F32, name="bias_rows_f32")
-        nc.vector.tensor_copy(out=bias_rows_f32[:], in_=bias_rows[:])
-        bias_ps = psum_work.tile([P, N_TILE], F32, name="bias_ps", tag="work")
-        nc.tensor.transpose(bias_ps[:, 0:P], bias_rows_f32[:], ident[:])
         bias_cols = const.tile([P, 3 * K_TILES], F32, name="bias_cols")
         nc.vector.tensor_copy(out=bias_cols[:], in_=bias_ps[:, 0 : 3 * K_TILES])
         phi_b_cols = bias_cols[:, 0:K_TILES]
@@ -154,27 +157,27 @@ def tile_attgcn_pa_kernel(
             w_scales[name] = const.tile([P, K], U8, name=name + "_scales", align_bytes=64)
         w_rows = {name: w_raw[name][:].rearrange("q (s n) -> q s n", s=PACK) for name in w_raw}
         w_copy = {"phi": nc.vector.tensor_copy, "theta": nc.scalar.copy}
-        th_t = const.tile([P, PASSES, ROWS, PACK], F32, name="th_t")
-        p_t = const.tile([P, PASSES, ROWS, PACK], F32, name="p_t")
-        p_mean = const.tile([P, PASSES, ROWS, PACK], F32, name="p_mean")
-        sum_p = []
+        sums = {}
         for g in range(PASSES):
             cols = slice(g * N_TILE, (g + 1) * N_TILE)
-            sums = {
-                "phi": psum_keep.tile([P, PACK, ROWS], F32, name="sum_p%d" % g),
-                "theta": psum_work.tile([P, PACK, ROWS], F32, name="sum_th", tag="work"),
+            sums[("phi", g)] = psum_keep.tile([P, PACK, ROWS], F32, name="sum_p%d" % g)
+            sums[("theta", g)] = psum_work.tile([P, PACK, ROWS], F32, name="sum_th", tag="work")
+            grouped = {
+                name: regroup_columns(w_copy[name], grouped_pool, w_rows[name][:, :, cols])
+                for name in ("phi", "theta")
             }
             for name in ("phi", "theta"):
-                quantise_columns(
-                    nc, w_copy[name], grouped_pool, w_rows[name][:, :, cols],
-                    w_codes[name][:, cols], w_scales[name][:, cols],
+                nc.vector.quantize_mx(
+                    out=w_codes[name][:, cols].bitcast(FP8X4), scales=w_scales[name][:, cols],
+                    in_=grouped[name][:],
                 )
+            for name in ("phi", "theta"):
                 for j in range(PACK):
                     tile_cols = slice((g * PACK + j) * P, (g * PACK + j + 1) * P)
                     for t in range(T):
                         step_cols = slice(t * ROWS, (t + 1) * ROWS)
                         nc.tensor.matmul_mx(
-                            out=sums[name][:, j, :],
+                            out=sums[(name, g)][:, j, :],
                             lhsT=w_codes[name][:, tile_cols].bitcast(FP8X4),
                             lhsT_scale=w_scales[name][:, tile_cols],
                             rhs=x_codes[:, step_cols].bitcast(FP8X4),
@@ -182,28 +185,7 @@ def tile_attgcn_pa_kernel(
                             start=(t == 0),
                             stop=(t == T - 1),
                         )
-            sum_p.append(sums["phi"])
-            nc.vector.tensor_copy(out=p_t[:, g, :, :], in_=sums["phi"][:].rearrange("q j r -> q r j"))
-            nc.scalar.mul(out=p_mean[:, g, :, :], in_=p_t[:, g, :, :], mul=1.0 / T)
-            nc.vector.tensor_tensor(
-                out=th_t[:, g, :, :],
-                in0=sums["theta"][:].rearrange("q j r -> q r j"),
-                in1=bias_diff_t[:, g * PACK : (g + 1) * PACK].unsqueeze(1).to_broadcast(
-                    [P, ROWS, PACK]
-                ),
-                op=ALU.add,
-            )
 
-        kappa_codes = const.tile([P, PASSES, K], U32, name="kappa_codes", align_bytes=64)
-        kappa_scales = const.tile([P, PASSES, K], U8, name="kappa_scales", align_bytes=64)
-        for g in range(PASSES):
-            rows = kappa_raw[g][:].rearrange("q (s n) -> q s n", s=PACK)
-            for half in range(K // N_TILE):
-                cols = slice(half * N_TILE, (half + 1) * N_TILE)
-                quantise_columns(
-                    nc, nc.scalar.copy, grouped_pool, rows[:, :, cols],
-                    kappa_codes[:, g, cols], kappa_scales[:, g, cols],
-                )
         a_plus = const.tile([P, K_TILES, V * V], F32, name="a_plus")
         for kt in range(K_TILES):
             nc.scalar.activation(
@@ -213,9 +195,41 @@ def tile_attgcn_pa_kernel(
                 bias=lam_kappa_b[:, kt : kt + 1],
             )
 
+        th_t = const.tile([P, PASSES, ROWS, PACK], F32, name="th_t")
+        p_t = const.tile([P, PASSES, ROWS, PACK], F32, name="p_t")
+        p_mean = const.tile([P, PASSES, ROWS, PACK], F32, name="p_mean")
+        kappa_codes = const.tile([P, PASSES, K], U32, name="kappa_codes", align_bytes=64)
+        kappa_scales = const.tile([P, PASSES, K], U8, name="kappa_scales", align_bytes=64)
         f_codes = {}
         f_scales = {}
         f_bf16 = {}
+
+        def take_sums_out(g):
+            nc.vector.tensor_tensor(
+                out=th_t[:, g, :, :],
+                in0=sums[("theta", g)][:].rearrange("q j r -> q r j"),
+                in1=bias_diff_t[:, g * PACK : (g + 1) * PACK].unsqueeze(1).to_broadcast(
+                    [P, ROWS, PACK]
+                ),
+                op=ALU.add,
+            )
+            nc.vector.tensor_copy(
+                out=p_t[:, g, :, :], in_=sums[("phi", g)][:].rearrange("q j r -> q r j")
+            )
+            nc.scalar.mul(out=p_mean[:, g, :, :], in_=p_t[:, g, :, :], mul=1.0 / T)
+
+        def quantise_kappa(g):
+            rows = kappa_raw[g][:].rearrange("q (s n) -> q s n", s=PACK)
+            halves = [slice(half * N_TILE, (half + 1) * N_TILE) for half in range(K // N_TILE)]
+            grouped = [
+                regroup_columns(nc.vector.tensor_copy, grouped_pool, rows[:, :, cols])
+                for cols in halves
+            ]
+            for cols, tile in zip(halves, grouped):
+                nc.vector.quantize_mx(
+                    out=kappa_codes[:, g, cols].bitcast(FP8X4), scales=kappa_scales[:, g, cols],
+                    in_=tile[:],
+                )
 
         def subtract_and_tanh(b, g, uc):
             first_u = b * V + uc * U_CHUNK
@@ -224,7 +238,7 @@ def tile_attgcn_pa_kernel(
             diff = diff_pool.tile([P, U_DIFF, V, PACK], F32, name="diff")
             nc.vector.tensor_tensor(
                 out=diff[:, 0:U_VECTOR, :, :],
-                in0=sum_p[g][:, :, first_u:split_u]
+                in0=sums[("phi", g)][:, :, first_u:split_u]
                 .rearrange("q j u -> q u j").unsqueeze(2).to_broadcast([P, U_VECTOR, V, PACK]),
                 in1=th_rows.unsqueeze(1).to_broadcast([P, U_VECTOR, V, PACK]),
                 op=ALU.subtract,
@@ -237,10 +251,6 @@ def tile_attgcn_pa_kernel(
                 op=ALU.subtract,
             )
             f = f_pool.tile([P, N_TILE * PACK], BF16, name="f", align_bytes=64)
-            nc.scalar.activation(
-                out=f[:, 0 : U_DIFF * V * PACK], in_=diff[:].rearrange("q u v j -> q (u v j)"),
-                func=ACT.Tanh, scale=1.0 / T,
-            )
             f_rows = f[:].rearrange("q (u v j) -> q u v j", v=V, j=PACK)
             for u in range(U_DIFF, U_CHUNK):
                 for j in range(PACK):
@@ -248,6 +258,10 @@ def tile_attgcn_pa_kernel(
                         out=f_rows[:, u, :, j], in_=th_rows[:, :, j], func=ACT.Tanh,
                         scale=-1.0 / T, bias=p_mean[:, g, first_u + u, j : j + 1],
                     )
+            nc.scalar.activation(
+                out=f[:, 0 : U_DIFF * V * PACK], in_=diff[:].rearrange("q u v j -> q (u v j)"),
+                func=ACT.Tanh, scale=1.0 / T,
+            )
             f_bf16[(b, g, uc)] = f
 
         def quantise_f(b, g, uc):
@@ -285,7 +299,12 @@ def tile_attgcn_pa_kernel(
         chunks = [(b, g, uc) for b in range(B) for g in range(PASSES) for uc in range(U_CHUNKS)]
         for step in range(len(chunks) + LAG + 1):
             if step < len(chunks):
-                subtract_and_tanh(*chunks[step])
+                b, g, uc = chunks[step]
+                if b == 0 and uc == 0:
+                    take_sums_out(g)
+                subtract_and_tanh(b, g, uc)
+                if b == 0 and uc == U_CHUNKS - 1:
+                    quantise_kappa(g)
             if 0 <= step - LAG < len(chunks):
                 quantise_f(*chunks[step - LAG])
             if 0 <= step - LAG - 1 < len(chunks):

@@ -21,12 +21,11 @@ K_TILES = K // P
 N_TILE = 512
 U_CHUNK = N_TILE // V
 U_CHUNKS = V // U_CHUNK
+CHUNKS = B * U_CHUNKS
+PIECES = N_TILE // P
+KINDS = 4
 RUN = 4
-LAG = 2
-U_GPSIMD = 5
-U_SCALAR = 3
-U_VECTOR = U_CHUNK - U_GPSIMD - U_SCALAR
-U_DIFF = U_VECTOR + U_GPSIMD
+QUANT_LAG = 2
 
 FLOPS = 2 * (B * T * V) * C * K * 2 + 2 * (B * V * V) * K * K
 
@@ -46,14 +45,13 @@ def tile_attgcn_pa_kernel(
     nc = tc.nc
     with ExitStack() as stack:
         const = stack.enter_context(tc.tile_pool(name="const", bufs=1))
-        raw_pool = stack.enter_context(tc.tile_pool(name="raw", bufs=5))
-        grouped_pool = stack.enter_context(tc.tile_pool(name="grouped", bufs=3))
-        diff_pool = stack.enter_context(tc.tile_pool(name="diff", bufs=4))
+        raw_pool = stack.enter_context(tc.tile_pool(name="raw", bufs=7))
+        grouped_pool = stack.enter_context(tc.tile_pool(name="grouped", bufs=4))
         f_pool = stack.enter_context(tc.tile_pool(name="f", bufs=4))
-        f_mx_pool = stack.enter_context(tc.tile_pool(name="f_mx", bufs=8))
-        result_pool = stack.enter_context(tc.tile_pool(name="result", bufs=6))
-        psum_keep = stack.enter_context(tc.psum_pool(name="psum_keep", bufs=1))
-        psum_work = stack.enter_context(tc.psum_pool(name="psum_work", bufs=6))
+        f_mx_pool = stack.enter_context(tc.tile_pool(name="f_mx", bufs=6))
+        result_pool = stack.enter_context(tc.tile_pool(name="result", bufs=8))
+        psum_diff = stack.enter_context(tc.psum_pool(name="psum_diff", bufs=4))
+        psum_acc = stack.enter_context(tc.psum_pool(name="psum_acc", bufs=4))
         stack.enter_context(tc.manual_schedule())
 
         bias_rows = const.tile([P, P], BF16, name="bias_rows")
@@ -92,22 +90,37 @@ def tile_attgcn_pa_kernel(
             nc.sync.dma_start(out=raw[:].rearrange("q (s n) -> q s n", s=PACK), in_=view)
             return raw
 
-        a_view = A.rearrange("(a q) u v -> q a (u v)", q=P)
-        a_raw = [
-            load_four_rows("a_raw%d" % half, a_view[:, half * PACK : (half + 1) * PACK, :])
-            for half in range(K_TILES // PACK)
-        ]
         kappa_view = kappa_w.rearrange("(a q) n -> q a n", q=P)
         kappa_raw = [
             load_four_rows("kappa_raw%d" % g, kappa_view[:, g * PACK : (g + 1) * PACK, :])
             for g in range(PASSES)
         ]
+        a_view = A.rearrange("(a q) u v -> q a (u v)", q=P)
+        a_raw = [
+            load_four_rows("a_raw%d" % half, a_view[:, half * PACK : (half + 1) * PACK, :])
+            for half in range(K_TILES // PACK)
+        ]
 
         ident = const.tile([P, P], F32, name="ident")
         make_identity(nc, ident[:])
+        ident_bf = const.tile([P, P], BF16, name="ident_bf")
+        nc.vector.tensor_copy(out=ident_bf[:], in_=ident[:])
 
         bias_rows_f32 = const.tile([P, P], F32, name="bias_rows_f32")
         nc.vector.tensor_copy(out=bias_rows_f32[:], in_=bias_rows[:])
+
+        is_u = const.tile([P, V], F32, name="is_u")
+        nc.vector.tensor_add(out=is_u[:], in0=ident[:, 0:V], in1=ident[:, V : 2 * V])
+        is_v = const.tile([P, V], F32, name="is_v")
+        nc.vector.tensor_add(out=is_v[:], in0=ident[:, 2 * V : 3 * V], in1=ident[:, 3 * V : 4 * V])
+        choose = const.tile([P, V, V], BF16, name="choose")
+        nc.vector.tensor_tensor(
+            out=choose[:],
+            in0=is_u[:].unsqueeze(2).to_broadcast([P, V, V]),
+            in1=is_v[:].unsqueeze(1).to_broadcast([P, V, V]),
+            op=ALU.subtract,
+        )
+        choose_cols = choose[:].rearrange("p u v -> p (u v)")
 
         x_words = x_raw[:].bitcast(F32)
         x_grouped = const.tile([P, T * ROWS * PACK], BF16, name="x_grouped", align_bytes=64)
@@ -116,7 +129,7 @@ def tile_attgcn_pa_kernel(
         )
         words = C // 2
         for b in range(B):
-            x_t = psum_work.tile([P, 2, 2 * P], F32, name="x_t", tag="work")
+            x_t = psum_diff.tile([P, 2, 2 * P], F32, name="x_t", tag="diff")
             for h in range(2):
                 for th in range(2):
                     first = (2 * b + th) * words + h * P
@@ -128,27 +141,12 @@ def tile_attgcn_pa_kernel(
                 out=x_grouped_words[:, :, b, :, :],
                 in_=x_t[:].rearrange("q h (t v) -> q t v h", v=V),
             )
-        bias_ps = psum_work.tile([P, N_TILE], F32, name="bias_ps", tag="work")
+        bias_ps = psum_diff.tile([P, N_TILE], F32, name="bias_ps", tag="diff")
         nc.tensor.transpose(bias_ps[:, 0:P], bias_rows_f32[:], ident[:])
 
         x_codes = const.tile([P, T * ROWS], U32, name="x_codes", align_bytes=64)
         x_scales = const.tile([P, T * ROWS], U8, name="x_scales", align_bytes=64)
         nc.vector.quantize_mx(out=x_codes[:].bitcast(FP8X4), scales=x_scales[:], in_=x_grouped[:])
-
-        bias_cols = const.tile([P, 3 * K_TILES], F32, name="bias_cols")
-        nc.vector.tensor_copy(out=bias_cols[:], in_=bias_ps[:, 0 : 3 * K_TILES])
-        phi_b_cols = bias_cols[:, 0:K_TILES]
-        theta_b_cols = bias_cols[:, K_TILES : 2 * K_TILES]
-        kappa_b_cols = bias_cols[:, 2 * K_TILES : 3 * K_TILES]
-
-        bias_diff = const.tile([P, K_TILES], F32, name="bias_diff")
-        nc.vector.tensor_sub(out=bias_diff[:], in0=theta_b_cols, in1=phi_b_cols)
-        bias_diff_t = const.tile([P, K_TILES], F32, name="bias_diff_t")
-        nc.vector.tensor_scalar_mul(out=bias_diff_t[:], in0=bias_diff[:], scalar1=float(T))
-        lam_col = const.tile([P, 1], F32, name="lam_col")
-        nc.vector.tensor_copy(out=lam_col[:], in_=lam_bf[:])
-        lam_kappa_b = const.tile([P, K_TILES], F32, name="lam_kappa_b")
-        nc.vector.tensor_scalar_mul(out=lam_kappa_b[:], in0=kappa_b_cols, scalar1=lam_col[:, 0:1])
 
         w_codes = {}
         w_scales = {}
@@ -157,11 +155,9 @@ def tile_attgcn_pa_kernel(
             w_scales[name] = const.tile([P, K], U8, name=name + "_scales", align_bytes=64)
         w_rows = {name: w_raw[name][:].rearrange("q (s n) -> q s n", s=PACK) for name in w_raw}
         w_copy = {"phi": nc.vector.tensor_copy, "theta": nc.scalar.copy}
-        sums = {}
-        for g in range(PASSES):
+
+        def quantise_weights(g):
             cols = slice(g * N_TILE, (g + 1) * N_TILE)
-            sums[("phi", g)] = psum_keep.tile([P, PACK, ROWS], F32, name="sum_p%d" % g)
-            sums[("theta", g)] = psum_work.tile([P, PACK, ROWS], F32, name="sum_th", tag="work")
             grouped = {
                 name: regroup_columns(w_copy[name], grouped_pool, w_rows[name][:, :, cols])
                 for name in ("phi", "theta")
@@ -171,143 +167,231 @@ def tile_attgcn_pa_kernel(
                     out=w_codes[name][:, cols].bitcast(FP8X4), scales=w_scales[name][:, cols],
                     in_=grouped[name][:],
                 )
-            for name in ("phi", "theta"):
-                for j in range(PACK):
-                    tile_cols = slice((g * PACK + j) * P, (g * PACK + j + 1) * P)
-                    for t in range(T):
-                        step_cols = slice(t * ROWS, (t + 1) * ROWS)
-                        nc.tensor.matmul_mx(
-                            out=sums[(name, g)][:, j, :],
-                            lhsT=w_codes[name][:, tile_cols].bitcast(FP8X4),
-                            lhsT_scale=w_scales[name][:, tile_cols],
-                            rhs=x_codes[:, step_cols].bitcast(FP8X4),
-                            rhs_scale=x_scales[:, step_cols],
-                            start=(t == 0),
-                            stop=(t == T - 1),
-                        )
+
+        quantise_weights(0)
+
+        bias_cols = const.tile([P, 3 * K_TILES], F32, name="bias_cols")
+        nc.vector.tensor_copy(out=bias_cols[:], in_=bias_ps[:, 0 : 3 * K_TILES])
+        phi_b_cols = bias_cols[:, 0:K_TILES]
+        theta_b_cols = bias_cols[:, K_TILES : 2 * K_TILES]
+        kappa_b_cols = bias_cols[:, 2 * K_TILES : 3 * K_TILES]
+        bias_diff = const.tile([P, K_TILES], F32, name="bias_diff")
+        nc.vector.tensor_sub(out=bias_diff[:], in0=phi_b_cols, in1=theta_b_cols)
+        lam_col = const.tile([P, 1], F32, name="lam_col")
+        nc.vector.tensor_copy(out=lam_col[:], in_=lam_bf[:])
+        bias_diff_t = const.tile([P, K_TILES], F32, name="bias_diff_t")
+        nc.vector.tensor_scalar_mul(out=bias_diff_t[:], in0=bias_diff[:], scalar1=float(T))
+        lam_kappa_b = const.tile([P, K_TILES], F32, name="lam_kappa_b")
+        nc.vector.tensor_scalar_mul(out=lam_kappa_b[:], in0=kappa_b_cols, scalar1=lam_col[:, 0:1])
+
+        quantise_weights(1)
 
         a_plus = const.tile([P, K_TILES, V * V], F32, name="a_plus")
-        for kt in range(K_TILES):
-            nc.scalar.activation(
-                out=a_plus[:, kt, :],
-                in_=a_raw[kt // PACK][:, (kt % PACK) * V * V : (kt % PACK + 1) * V * V],
-                func=ACT.Identity,
-                bias=lam_kappa_b[:, kt : kt + 1],
-            )
+        for uc in range(U_CHUNKS):
+            for kt in range(K_TILES):
+                first = (kt % PACK) * V * V + uc * N_TILE
+                nc.gpsimd.tensor_scalar(
+                    out=a_plus[:, kt, uc * N_TILE : (uc + 1) * N_TILE],
+                    in0=a_raw[kt // PACK][:, first : first + N_TILE],
+                    scalar1=1.0, scalar2=lam_kappa_b[:, kt : kt + 1],
+                    op0=ALU.mult, op1=ALU.add,
+                )
 
-        th_t = const.tile([P, PASSES, ROWS, PACK], F32, name="th_t")
-        p_t = const.tile([P, PASSES, ROWS, PACK], F32, name="p_t")
-        p_mean = const.tile([P, PASSES, ROWS, PACK], F32, name="p_mean")
-        kappa_codes = const.tile([P, PASSES, K], U32, name="kappa_codes", align_bytes=64)
-        kappa_scales = const.tile([P, PASSES, K], U8, name="kappa_scales", align_bytes=64)
-        f_codes = {}
-        f_scales = {}
-        f_bf16 = {}
+        sums = {}
 
-        def take_sums_out(g):
+        def open_sums(name, g):
+            sums[(name, g)] = psum_acc.tile([P, PACK, ROWS], F32, name="sum", tag="acc")
+
+        def sum_over_time(name, g, j):
+            tile_cols = slice((g * PACK + j) * P, (g * PACK + j + 1) * P)
+            for t in range(T):
+                step_cols = slice(t * ROWS, (t + 1) * ROWS)
+                nc.tensor.matmul_mx(
+                    out=sums[(name, g)][:, j, :],
+                    lhsT=w_codes[name][:, tile_cols].bitcast(FP8X4),
+                    lhsT_scale=w_scales[name][:, tile_cols],
+                    rhs=x_codes[:, step_cols].bitcast(FP8X4),
+                    rhs_scale=x_scales[:, step_cols],
+                    start=(t == 0),
+                    stop=(t == T - 1),
+                )
+
+        halves = [
+            const.tile([P, PACK, B, KINDS, V], BF16, name="halves%d" % g, align_bytes=64)
+            for g in range(PASSES)
+        ]
+        p_biased = [const.tile([P, PACK, ROWS], F32, name="p_biased%d" % g) for g in range(PASSES)]
+
+        def add_bias(g):
             nc.vector.tensor_tensor(
-                out=th_t[:, g, :, :],
-                in0=sums[("theta", g)][:].rearrange("q j r -> q r j"),
-                in1=bias_diff_t[:, g * PACK : (g + 1) * PACK].unsqueeze(1).to_broadcast(
-                    [P, ROWS, PACK]
+                out=p_biased[g][:],
+                in0=sums[("phi", g)][:],
+                in1=bias_diff_t[:, g * PACK : (g + 1) * PACK].unsqueeze(2).to_broadcast(
+                    [P, PACK, ROWS]
                 ),
                 op=ALU.add,
             )
-            nc.vector.tensor_copy(
-                out=p_t[:, g, :, :], in_=sums[("phi", g)][:].rearrange("q j r -> q r j")
-            )
-            nc.scalar.mul(out=p_mean[:, g, :, :], in_=p_t[:, g, :, :], mul=1.0 / T)
 
-        def quantise_kappa(g):
-            rows = kappa_raw[g][:].rearrange("q (s n) -> q s n", s=PACK)
-            halves = [slice(half * N_TILE, (half + 1) * N_TILE) for half in range(K // N_TILE)]
-            grouped = [
-                regroup_columns(nc.vector.tensor_copy, grouped_pool, rows[:, :, cols])
-                for cols in halves
-            ]
-            for cols, tile in zip(halves, grouped):
-                nc.vector.quantize_mx(
-                    out=kappa_codes[:, g, cols].bitcast(FP8X4), scales=kappa_scales[:, g, cols],
-                    in_=tile[:],
-                )
+        def whole(name, g):
+            tile = p_biased[g] if name == "phi" else sums[("theta", g)]
+            return tile[:].rearrange("q j (b w) -> q j b w", b=B)
 
-        def subtract_and_tanh(b, g, uc):
-            first_u = b * V + uc * U_CHUNK
-            split_u = first_u + U_VECTOR
-            th_rows = th_t[:, g, b * V : (b + 1) * V, :]
-            diff = diff_pool.tile([P, U_DIFF, V, PACK], F32, name="diff")
+        def high_half(name, g):
+            kind = 0 if name == "phi" else 2
+            nc.scalar.copy(out=halves[g][:, :, :, kind, :], in_=whole(name, g))
+
+        def low_half(name, g):
+            kind = 0 if name == "phi" else 2
             nc.vector.tensor_tensor(
-                out=diff[:, 0:U_VECTOR, :, :],
-                in0=sums[("phi", g)][:, :, first_u:split_u]
-                .rearrange("q j u -> q u j").unsqueeze(2).to_broadcast([P, U_VECTOR, V, PACK]),
-                in1=th_rows.unsqueeze(1).to_broadcast([P, U_VECTOR, V, PACK]),
+                out=halves[g][:, :, :, kind + 1, :],
+                in0=whole(name, g),
+                in1=halves[g][:, :, :, kind, :],
                 op=ALU.subtract,
             )
-            nc.gpsimd.tensor_tensor(
-                out=diff[:, U_VECTOR:U_DIFF, :, :],
-                in0=p_t[:, g, split_u : first_u + U_DIFF, :]
-                .unsqueeze(2).to_broadcast([P, U_GPSIMD, V, PACK]),
-                in1=th_rows.unsqueeze(1).to_broadcast([P, U_GPSIMD, V, PACK]),
-                op=ALU.subtract,
-            )
-            f = f_pool.tile([P, N_TILE * PACK], BF16, name="f", align_bytes=64)
-            f_rows = f[:].rearrange("q (u v j) -> q u v j", v=V, j=PACK)
-            for u in range(U_DIFF, U_CHUNK):
-                for j in range(PACK):
-                    nc.scalar.activation(
-                        out=f_rows[:, u, :, j], in_=th_rows[:, :, j], func=ACT.Tanh,
-                        scale=-1.0 / T, bias=p_mean[:, g, first_u + u, j : j + 1],
-                    )
+
+        turned = {}
+
+        def turn_halves(g, b):
+            bank = psum_diff.tile([P, 2 * N_TILE], BF16, name="turn_ps", tag="diff")
+            for j in range(PACK):
+                nc.tensor.transpose(
+                    bank[:, j * P : (j + 1) * P],
+                    halves[g][:, j, b, :, :].rearrange("q k w -> q (k w)"),
+                    ident_bf[:],
+                )
+            tile = const.tile([P, N_TILE], BF16, name="turned_%d_%d" % (g, b), align_bytes=64)
+            nc.scalar.copy(out=tile[:], in_=bank[:, 0:N_TILE])
+            turned[(g, b)] = tile
+
+        f_bf16 = {}
+        f_codes = {}
+        f_scales = {}
+
+        def difference_and_tanh(c, g, n):
+            b, uc = divmod(c, U_CHUNKS)
+            if n == 0:
+                f_bf16[(c, g)] = f_pool.tile([P, N_TILE * PACK], BF16, name="f", align_bytes=64)
+            first = (uc * PIECES + n) * P
+            bank = psum_diff.tile([P, PACK, P], F32, name="diff_ps", tag="diff")
+            for j in range(PACK):
+                nc.tensor.matmul(
+                    bank[:, j, :],
+                    lhsT=turned[(g, b)][:, j * P : (j + 1) * P],
+                    rhs=choose_cols[:, first : first + P],
+                    start=True,
+                    stop=True,
+                )
             nc.scalar.activation(
-                out=f[:, 0 : U_DIFF * V * PACK], in_=diff[:].rearrange("q u v j -> q (u v j)"),
+                out=f_bf16[(c, g)][:, n * N_TILE : (n + 1) * N_TILE].rearrange(
+                    "q (m j) -> q m j", j=PACK
+                ),
+                in_=bank[:].rearrange("q j m -> q m j"),
                 func=ACT.Tanh, scale=1.0 / T,
             )
-            f_bf16[(b, g, uc)] = f
 
-        def quantise_f(b, g, uc):
+        def quantise_f(c, g):
             codes = f_mx_pool.tile([P, N_TILE], U32, name="f_codes", align_bytes=64)
             scales = f_mx_pool.tile([P, N_TILE], U8, name="f_scales", align_bytes=64)
             nc.vector.quantize_mx(
-                out=codes[:].bitcast(FP8X4), scales=scales[:], in_=f_bf16[(b, g, uc)][:]
+                out=codes[:].bitcast(FP8X4), scales=scales[:], in_=f_bf16[(c, g)][:]
             )
-            f_codes[(b, g, uc)] = codes
-            f_scales[(b, g, uc)] = scales
+            f_codes[(c, g)] = codes
+            f_scales[(c, g)] = scales
 
-        def multiply_and_store(b, uc):
+        kappa_codes = const.tile([P, PASSES, K], U32, name="kappa_codes", align_bytes=64)
+        kappa_scales = const.tile([P, PASSES, K], U8, name="kappa_scales", align_bytes=64)
+        kappa_grouped = {}
+
+        def regroup_kappa(g, half):
+            rows = kappa_raw[g][:].rearrange("q (s n) -> q s n", s=PACK)
+            cols = slice(half * N_TILE, (half + 1) * N_TILE)
+            kappa_grouped[(g, half)] = regroup_columns(
+                nc.vector.tensor_copy, grouped_pool, rows[:, :, cols]
+            )
+
+        def quantise_kappa(g, half):
+            cols = slice(half * N_TILE, (half + 1) * N_TILE)
+            nc.vector.quantize_mx(
+                out=kappa_codes[:, g, cols].bitcast(FP8X4), scales=kappa_scales[:, g, cols],
+                in_=kappa_grouped[(g, half)][:],
+            )
+
+        def multiply_and_store(c, kt):
+            b, uc = divmod(c, U_CHUNKS)
             cols = slice(uc * N_TILE, (uc + 1) * N_TILE)
-            out_view = out[b].rearrange("(a q) u v -> q a (u v)", q=P)
-            for kt in range(K_TILES):
-                tile_cols = slice(kt * P, (kt + 1) * P)
-                acc = psum_work.tile([P, N_TILE], F32, name="acc", tag="work")
-                for g in range(PASSES):
-                    nc.tensor.matmul_mx(
-                        out=acc[:],
-                        lhsT=kappa_codes[:, g, tile_cols].bitcast(FP8X4),
-                        lhsT_scale=kappa_scales[:, g, tile_cols],
-                        rhs=f_codes[(b, g, uc)][:].bitcast(FP8X4),
-                        rhs_scale=f_scales[(b, g, uc)][:],
-                        start=(g == 0),
-                        stop=(g == PASSES - 1),
-                    )
-                result = result_pool.tile([P, N_TILE], F32, name="result")
-                nc.vector.scalar_tensor_tensor(
-                    out=result[:], in0=acc[:], scalar=lam_col[:, 0:1], in1=a_plus[:, kt, cols],
-                    op0=ALU.mult, op1=ALU.add,
+            tile_cols = slice(kt * P, (kt + 1) * P)
+            acc = psum_acc.tile([P, N_TILE], F32, name="acc", tag="acc")
+            for g in range(PASSES):
+                nc.tensor.matmul_mx(
+                    out=acc[:],
+                    lhsT=kappa_codes[:, g, tile_cols].bitcast(FP8X4),
+                    lhsT_scale=kappa_scales[:, g, tile_cols],
+                    rhs=f_codes[(c, g)][:].bitcast(FP8X4),
+                    rhs_scale=f_scales[(c, g)][:],
+                    start=(g == 0),
+                    stop=(g == PASSES - 1),
                 )
-                nc.sync.dma_start(out=out_view[:, kt, cols], in_=result[:])
+            result = result_pool.tile([P, N_TILE], F32, name="result")
+            nc.vector.scalar_tensor_tensor(
+                out=result[:], in0=acc[:], scalar=lam_col[:, 0:1], in1=a_plus[:, kt, cols],
+                op0=ALU.mult, op1=ALU.add,
+            )
+            out_view = out[b].rearrange("(a q) u v -> q a (u v)", q=P)
+            nc.sync.dma_start(out=out_view[:, kt, cols], in_=result[:])
 
-        chunks = [(b, g, uc) for b in range(B) for g in range(PASSES) for uc in range(U_CHUNKS)]
-        for step in range(len(chunks) + LAG + 1):
-            if step < len(chunks):
-                b, g, uc = chunks[step]
-                if b == 0 and uc == 0:
-                    take_sums_out(g)
-                subtract_and_tanh(b, g, uc)
-                if b == 0 and uc == U_CHUNKS - 1:
-                    quantise_kappa(g)
-            if 0 <= step - LAG < len(chunks):
-                quantise_f(*chunks[step - LAG])
-            if 0 <= step - LAG - 1 < len(chunks):
-                b, g, uc = chunks[step - LAG - 1]
-                if g == PASSES - 1:
-                    multiply_and_store(b, uc)
+        for name, g in (("phi", 0), ("theta", 0), ("phi", 1)):
+            open_sums(name, g)
+            for j in range(PACK):
+                sum_over_time(name, g, j)
+        add_bias(0)
+        high_half("phi", 0)
+        regroup_kappa(0, 0)
+        low_half("phi", 0)
+        high_half("theta", 0)
+        regroup_kappa(0, 1)
+        low_half("theta", 0)
+        turn_halves(0, 0)
+        add_bias(1)
+        high_half("phi", 1)
+        quantise_kappa(0, 0)
+        low_half("phi", 1)
+        quantise_kappa(0, 1)
+        open_sums("theta", 1)
+        for j in range(PACK):
+            sum_over_time("theta", 1, j)
+            if j < PACK - 1:
+                difference_and_tanh(0, 0, j)
+        high_half("theta", 1)
+        difference_and_tanh(0, 0, PIECES - 1)
+        regroup_kappa(1, 0)
+        low_half("theta", 1)
+        difference_and_tanh(1, 0, 0)
+        difference_and_tanh(1, 0, 1)
+        turn_halves(1, 0)
+        regroup_kappa(1, 1)
+        quantise_kappa(1, 0)
+        difference_and_tanh(1, 0, 2)
+        difference_and_tanh(1, 0, 3)
+        quantise_f(0, 0)
+        quantise_kappa(1, 1)
+        for n in range(PIECES):
+            difference_and_tanh(0, 1, n)
+        quantise_f(1, 0)
+        quantise_f(0, 1)
+
+        ahead = [(1, 1, n) for n in range(PIECES)]
+        for c in range(U_CHUNKS, CHUNKS):
+            ahead += [(c, g, n) for g in range(PASSES) for n in range(PIECES)]
+        to_turn = [(g, b) for b in range(1, B) for g in range(PASSES)]
+        to_quantise = {}
+        for item in range(CHUNKS * K_TILES):
+            multiply_and_store(*divmod(item, K_TILES))
+            if 0 <= item - 1 < len(to_turn):
+                turn_halves(*to_turn[item - 1])
+            if item < len(ahead):
+                c, g, n = ahead[item]
+                difference_and_tanh(c, g, n)
+                if n == PIECES - 1:
+                    to_quantise[item + QUANT_LAG] = (c, g)
+            if item in to_quantise:
+                quantise_f(*to_quantise[item])

@@ -25,7 +25,8 @@ CHUNKS = B * U_CHUNKS
 PIECES = N_TILE // P
 KINDS = 4
 RUN = 4
-QUANT_LAG = 2
+U_GPSIMD = 4
+QUANT_LAG = 1
 
 FLOPS = 2 * (B * T * V) * C * K * 2 + 2 * (B * V * V) * K * K
 
@@ -47,7 +48,8 @@ def tile_attgcn_pa_kernel(
         const = stack.enter_context(tc.tile_pool(name="const", bufs=1))
         raw_pool = stack.enter_context(tc.tile_pool(name="raw", bufs=7))
         grouped_pool = stack.enter_context(tc.tile_pool(name="grouped", bufs=4))
-        f_pool = stack.enter_context(tc.tile_pool(name="f", bufs=4))
+        f_pool = stack.enter_context(tc.tile_pool(name="f", bufs=5))
+        diff_pool = stack.enter_context(tc.tile_pool(name="diff", bufs=4))
         f_mx_pool = stack.enter_context(tc.tile_pool(name="f_mx", bufs=6))
         result_pool = stack.enter_context(tc.tile_pool(name="result", bufs=8))
         psum_diff = stack.enter_context(tc.psum_pool(name="psum_diff", bufs=4))
@@ -70,9 +72,8 @@ def tile_attgcn_pa_kernel(
         x_raw = raw_tile("x_raw")
         x_rows = x_raw[:].rearrange("p (n c) -> p n c", c=C)
         x_view = x.flatten_outer_dims().rearrange("(n p) c -> p n c", p=P)
-        for half in range(2):
-            tiles = slice(half * X_TILES // 2, (half + 1) * X_TILES // 2)
-            nc.sync.dma_start(out=x_rows[:, tiles, :], in_=x_view[:, tiles, :])
+        for th in range(2):
+            nc.sync.dma_start(out=x_rows[:, th::2, :], in_=x_view[:, th::2, :])
 
         w_raw = {"phi": raw_tile("phi_raw"), "theta": raw_tile("theta_raw")}
         w_dram = {"phi": phi_w, "theta": theta_w}
@@ -85,21 +86,19 @@ def tile_attgcn_pa_kernel(
                         in_=w_dram[name].rearrange("(h q e) n -> q h e n", h=2, e=2)[:, h, :, cols],
                     )
 
-        def load_four_rows(name, view):
-            raw = raw_tile(name)
-            nc.sync.dma_start(out=raw[:].rearrange("q (s n) -> q s n", s=PACK), in_=view)
-            return raw
-
-        kappa_view = kappa_w.rearrange("(a q) n -> q a n", q=P)
-        kappa_raw = [
-            load_four_rows("kappa_raw%d" % g, kappa_view[:, g * PACK : (g + 1) * PACK, :])
-            for g in range(PASSES)
-        ]
         a_view = A.rearrange("(a q) u v -> q a (u v)", q=P)
-        a_raw = [
-            load_four_rows("a_raw%d" % half, a_view[:, half * PACK : (half + 1) * PACK, :])
-            for half in range(K_TILES // PACK)
-        ]
+        kappa_view = kappa_w.rearrange("(a q) n -> q a n", q=P)
+        a_raw = []
+        kappa_raw = []
+        for raws, name, view, half in (
+            (kappa_raw, "kappa_raw0", kappa_view, 0),
+            (a_raw, "a_raw0", a_view, 0),
+            (kappa_raw, "kappa_raw1", kappa_view, 1),
+            (a_raw, "a_raw1", a_view, 1),
+        ):
+            raw = raw_tile(name)[:].rearrange("q (a n) -> q a n", n=N_TILE)
+            nc.sync.dma_start(out=raw, in_=view[:, :, half * N_TILE : (half + 1) * N_TILE])
+            raws.append(raw)
 
         ident = const.tile([P, P], F32, name="ident")
         make_identity(nc, ident[:])
@@ -107,7 +106,6 @@ def tile_attgcn_pa_kernel(
         nc.vector.tensor_copy(out=ident_bf[:], in_=ident[:])
 
         bias_rows_f32 = const.tile([P, P], F32, name="bias_rows_f32")
-        nc.vector.tensor_copy(out=bias_rows_f32[:], in_=bias_rows[:])
 
         is_u = const.tile([P, V], F32, name="is_u")
         nc.vector.tensor_add(out=is_u[:], in0=ident[:, 0:V], in1=ident[:, V : 2 * V])
@@ -128,25 +126,38 @@ def tile_attgcn_pa_kernel(
             "q (t b v h) -> q t b v h", t=T, b=B, v=V
         )
         words = C // 2
-        for b in range(B):
-            x_t = psum_diff.tile([P, 2, 2 * P], F32, name="x_t", tag="diff")
-            for h in range(2):
-                for th in range(2):
-                    first = (2 * b + th) * words + h * P
-                    nc.tensor.transpose(
-                        x_t[:, h, th * P : (th + 1) * P], x_words[:, first : first + P], ident[:]
-                    )
-            copy = nc.vector.tensor_copy if b % 2 == 0 else nc.scalar.copy
-            copy(
-                out=x_grouped_words[:, :, b, :, :],
-                in_=x_t[:].rearrange("q h (t v) -> q t v h", v=V),
-            )
-        bias_ps = psum_diff.tile([P, N_TILE], F32, name="bias_ps", tag="diff")
-        nc.tensor.transpose(bias_ps[:, 0:P], bias_rows_f32[:], ident[:])
-
         x_codes = const.tile([P, T * ROWS], U32, name="x_codes", align_bytes=64)
         x_scales = const.tile([P, T * ROWS], U8, name="x_scales", align_bytes=64)
-        nc.vector.quantize_mx(out=x_codes[:].bitcast(FP8X4), scales=x_scales[:], in_=x_grouped[:])
+
+        def turn_x(th):
+            for pair in range(B // 2):
+                x_t = psum_diff.tile([P, 2, 2, P], F32, name="x_t", tag="diff")
+                for i in range(2):
+                    for h in range(2):
+                        first = (2 * (2 * pair + i) + th) * words + h * P
+                        nc.tensor.transpose(
+                            x_t[:, i, h, :], x_words[:, first : first + P], ident[:]
+                        )
+                copy = nc.vector.tensor_copy if th == 0 else nc.scalar.copy
+                for i in range(2):
+                    copy(
+                        out=x_grouped_words[:, th * T // 2 : (th + 1) * T // 2, 2 * pair + i, :, :],
+                        in_=x_t[:, i, :, :].rearrange("q h (t v) -> q t v h", v=V),
+                    )
+
+        def quantise_x(th):
+            cols = slice(th * T * ROWS // 2, (th + 1) * T * ROWS // 2)
+            nc.vector.quantize_mx(
+                out=x_codes[:, cols].bitcast(FP8X4), scales=x_scales[:, cols],
+                in_=x_grouped[:, th * T * ROWS * PACK // 2 : (th + 1) * T * ROWS * PACK // 2],
+            )
+
+        turn_x(0)
+        turn_x(1)
+        nc.vector.tensor_copy(out=bias_rows_f32[:], in_=bias_rows[:])
+        quantise_x(0)
+        bias_ps = psum_diff.tile([P, N_TILE], F32, name="bias_ps", tag="diff")
+        nc.tensor.transpose(bias_ps[:, 0:P], bias_rows_f32[:], ident[:])
 
         w_codes = {}
         w_scales = {}
@@ -156,19 +167,29 @@ def tile_attgcn_pa_kernel(
         w_rows = {name: w_raw[name][:].rearrange("q (s n) -> q s n", s=PACK) for name in w_raw}
         w_copy = {"phi": nc.vector.tensor_copy, "theta": nc.scalar.copy}
 
-        def quantise_weights(g):
-            cols = slice(g * N_TILE, (g + 1) * N_TILE)
-            grouped = {
-                name: regroup_columns(w_copy[name], grouped_pool, w_rows[name][:, :, cols])
-                for name in ("phi", "theta")
-            }
-            for name in ("phi", "theta"):
-                nc.vector.quantize_mx(
-                    out=w_codes[name][:, cols].bitcast(FP8X4), scales=w_scales[name][:, cols],
-                    in_=grouped[name][:],
-                )
+        w_grouped = {}
 
-        quantise_weights(0)
+        def regroup_weights(name, g):
+            cols = slice(g * N_TILE, (g + 1) * N_TILE)
+            w_grouped[(name, g)] = regroup_columns(
+                w_copy[name], grouped_pool, w_rows[name][:, :, cols]
+            )
+
+        def quantise_weights(name, g):
+            cols = slice(g * N_TILE, (g + 1) * N_TILE)
+            nc.vector.quantize_mx(
+                out=w_codes[name][:, cols].bitcast(FP8X4), scales=w_scales[name][:, cols],
+                in_=w_grouped[(name, g)][:],
+            )
+
+        regroup_weights("phi", 0)
+        regroup_weights("theta", 0)
+        quantise_x(1)
+        quantise_weights("phi", 0)
+
+        regroup_weights("phi", 1)
+        quantise_weights("theta", 0)
+        regroup_weights("theta", 1)
 
         bias_cols = const.tile([P, 3 * K_TILES], F32, name="bias_cols")
         nc.vector.tensor_copy(out=bias_cols[:], in_=bias_ps[:, 0 : 3 * K_TILES])
@@ -184,15 +205,20 @@ def tile_attgcn_pa_kernel(
         lam_kappa_b = const.tile([P, K_TILES], F32, name="lam_kappa_b")
         nc.vector.tensor_scalar_mul(out=lam_kappa_b[:], in0=kappa_b_cols, scalar1=lam_col[:, 0:1])
 
-        quantise_weights(1)
+        quantise_weights("phi", 1)
+        quantise_weights("theta", 1)
 
-        a_plus = const.tile([P, K_TILES, V * V], F32, name="a_plus")
-        for uc in range(U_CHUNKS):
-            for kt in range(K_TILES):
-                first = (kt % PACK) * V * V + uc * N_TILE
+        a_plus = const.tile([P, U_CHUNKS, K_TILES, N_TILE], F32, name="a_plus")
+
+        def prepare_a(uc, kt):
+            if uc == 0:
+                nc.scalar.activation(
+                    out=a_plus[:, uc, kt, :], in_=a_raw[uc][:, kt, :], func=ACT.Identity,
+                    bias=lam_kappa_b[:, kt : kt + 1],
+                )
+            else:
                 nc.gpsimd.tensor_scalar(
-                    out=a_plus[:, kt, uc * N_TILE : (uc + 1) * N_TILE],
-                    in0=a_raw[kt // PACK][:, first : first + N_TILE],
+                    out=a_plus[:, uc, kt, :], in0=a_raw[uc][:, kt, :],
                     scalar1=1.0, scalar2=lam_kappa_b[:, kt : kt + 1],
                     op0=ALU.mult, op1=ALU.add,
                 )
@@ -217,35 +243,37 @@ def tile_attgcn_pa_kernel(
                 )
 
         halves = [
-            const.tile([P, PACK, B, KINDS, V], BF16, name="halves%d" % g, align_bytes=64)
-            for g in range(PASSES)
+            const.tile([P, PACK, b_count, KINDS, V], BF16, name="halves", tag="halves%d" % b_count)
+            for b_count in (1, B)
         ]
-        p_biased = [const.tile([P, PACK, ROWS], F32, name="p_biased%d" % g) for g in range(PASSES)]
+        p_biased = const.tile([P, PASSES, PACK, ROWS], F32, name="p_biased")
 
-        def add_bias(g):
+        def add_bias(g, batches):
+            rows = slice(batches.start * V, batches.stop * V)
+            width = (batches.stop - batches.start) * V
             nc.vector.tensor_tensor(
-                out=p_biased[g][:],
-                in0=sums[("phi", g)][:],
+                out=p_biased[:, g, :, rows],
+                in0=sums[("phi", g)][:, :, rows],
                 in1=bias_diff_t[:, g * PACK : (g + 1) * PACK].unsqueeze(2).to_broadcast(
-                    [P, PACK, ROWS]
+                    [P, PACK, width]
                 ),
                 op=ALU.add,
             )
 
-        def whole(name, g):
-            tile = p_biased[g] if name == "phi" else sums[("theta", g)]
-            return tile[:].rearrange("q j (b w) -> q j b w", b=B)
+        def whole(name, g, batches):
+            tile = p_biased[:, g, :, :] if name == "phi" else sums[("theta", g)][:]
+            return tile.rearrange("q j (b w) -> q j b w", b=B)[:, :, batches, :]
 
-        def high_half(name, g):
+        def high_half(name, g, batches):
             kind = 0 if name == "phi" else 2
-            nc.scalar.copy(out=halves[g][:, :, :, kind, :], in_=whole(name, g))
+            nc.scalar.copy(out=halves[g][:, :, batches, kind, :], in_=whole(name, g, batches))
 
-        def low_half(name, g):
+        def low_half(name, g, batches):
             kind = 0 if name == "phi" else 2
             nc.vector.tensor_tensor(
-                out=halves[g][:, :, :, kind + 1, :],
-                in0=whole(name, g),
-                in1=halves[g][:, :, :, kind, :],
+                out=halves[g][:, :, batches, kind + 1, :],
+                in0=whole(name, g, batches),
+                in1=halves[g][:, :, batches, kind, :],
                 op=ALU.subtract,
             )
 
@@ -262,6 +290,48 @@ def tile_attgcn_pa_kernel(
             tile = const.tile([P, N_TILE], BF16, name="turned_%d_%d" % (g, b), align_bytes=64)
             nc.scalar.copy(out=tile[:], in_=bank[:, 0:N_TILE])
             turned[(g, b)] = tile
+
+        p_t = const.tile([P, ROWS, PACK], F32, name="p_t")
+        th_t = const.tile([P, ROWS, PACK], F32, name="th_t")
+        gpsimd_diff = {}
+
+        def take_out_p():
+            nc.vector.tensor_tensor(
+                out=p_t[:, V:, :],
+                in0=sums[("phi", 0)][:, :, V:].rearrange("q j r -> q r j"),
+                in1=bias_diff_t[:, 0:PACK].unsqueeze(1).to_broadcast([P, ROWS - V, PACK]),
+                op=ALU.add,
+            )
+
+        def take_out_th():
+            nc.vector.tensor_copy(
+                out=th_t[:, V:, :], in_=sums[("theta", 0)][:, :, V:].rearrange("q j r -> q r j")
+            )
+
+        def gpsimd_difference(c, half):
+            b, uc = divmod(c, U_CHUNKS)
+            diff = diff_pool.tile([P, U_CHUNK // 2, V, PACK], F32, name="diff")
+            for i in range(0, U_CHUNK // 2, U_GPSIMD):
+                first_u = b * V + uc * U_CHUNK + half * U_CHUNK // 2 + i
+                nc.gpsimd.tensor_tensor(
+                    out=diff[:, i : i + U_GPSIMD, :, :],
+                    in0=p_t[:, first_u : first_u + U_GPSIMD, :]
+                    .unsqueeze(2).to_broadcast([P, U_GPSIMD, V, PACK]),
+                    in1=th_t[:, b * V : (b + 1) * V, :]
+                    .unsqueeze(1).to_broadcast([P, U_GPSIMD, V, PACK]),
+                    op=ALU.subtract,
+                )
+            gpsimd_diff[(c, half)] = diff
+
+        def gpsimd_tanh(c, half):
+            if half == 0:
+                f_bf16[(c, 0)] = f_pool.tile([P, N_TILE * PACK], BF16, name="f", align_bytes=64)
+            width = N_TILE * PACK // 2
+            nc.scalar.activation(
+                out=f_bf16[(c, 0)][:, half * width : (half + 1) * width],
+                in_=gpsimd_diff[(c, half)][:].rearrange("q u v j -> q (u v j)"),
+                func=ACT.Tanh, scale=1.0 / T,
+            )
 
         f_bf16 = {}
         f_codes = {}
@@ -303,10 +373,8 @@ def tile_attgcn_pa_kernel(
         kappa_grouped = {}
 
         def regroup_kappa(g, half):
-            rows = kappa_raw[g][:].rearrange("q (s n) -> q s n", s=PACK)
-            cols = slice(half * N_TILE, (half + 1) * N_TILE)
             kappa_grouped[(g, half)] = regroup_columns(
-                nc.vector.tensor_copy, grouped_pool, rows[:, :, cols]
+                nc.vector.tensor_copy, grouped_pool, kappa_raw[half][:, g * PACK : (g + 1) * PACK, :]
             )
 
         def quantise_kappa(g, half):
@@ -333,65 +401,91 @@ def tile_attgcn_pa_kernel(
                 )
             result = result_pool.tile([P, N_TILE], F32, name="result")
             nc.vector.scalar_tensor_tensor(
-                out=result[:], in0=acc[:], scalar=lam_col[:, 0:1], in1=a_plus[:, kt, cols],
+                out=result[:], in0=acc[:], scalar=lam_col[:, 0:1], in1=a_plus[:, uc, kt, :],
                 op0=ALU.mult, op1=ALU.add,
             )
             out_view = out[b].rearrange("(a q) u v -> q a (u v)", q=P)
             nc.sync.dma_start(out=out_view[:, kt, cols], in_=result[:])
 
+        FIRST = slice(0, 1)
+        REST = slice(1, B)
+        ALL = slice(0, B)
         for name, g in (("phi", 0), ("theta", 0), ("phi", 1)):
             open_sums(name, g)
             for j in range(PACK):
                 sum_over_time(name, g, j)
-        add_bias(0)
-        high_half("phi", 0)
-        regroup_kappa(0, 0)
-        low_half("phi", 0)
-        high_half("theta", 0)
-        regroup_kappa(0, 1)
-        low_half("theta", 0)
-        turn_halves(0, 0)
-        add_bias(1)
-        high_half("phi", 1)
-        quantise_kappa(0, 0)
-        low_half("phi", 1)
-        quantise_kappa(0, 1)
         open_sums("theta", 1)
-        for j in range(PACK):
-            sum_over_time("theta", 1, j)
-            if j < PACK - 1:
-                difference_and_tanh(0, 0, j)
-        high_half("theta", 1)
-        difference_and_tanh(0, 0, PIECES - 1)
+        sum_over_time("theta", 1, 0)
+        regroup_kappa(0, 0)
+        add_bias(0, FIRST)
+        high_half("phi", 0, FIRST)
+        take_out_p()
+        low_half("phi", 0, FIRST)
+        for kt in range(3):
+            prepare_a(0, kt)
         regroup_kappa(1, 0)
-        low_half("theta", 1)
-        difference_and_tanh(1, 0, 0)
-        difference_and_tanh(1, 0, 1)
-        turn_halves(1, 0)
-        regroup_kappa(1, 1)
+        high_half("theta", 0, FIRST)
+        low_half("theta", 0, FIRST)
+        turn_halves(0, 0)
+        quantise_kappa(0, 0)
         quantise_kappa(1, 0)
-        difference_and_tanh(1, 0, 2)
-        difference_and_tanh(1, 0, 3)
-        quantise_f(0, 0)
+        for kt in range(3, 5):
+            prepare_a(0, kt)
+        regroup_kappa(0, 1)
+        add_bias(1, ALL)
+        high_half("phi", 1, ALL)
+        regroup_kappa(1, 1)
+        low_half("phi", 1, ALL)
+        quantise_kappa(0, 1)
         quantise_kappa(1, 1)
+        sum_over_time("theta", 1, 1)
+        difference_and_tanh(0, 0, 0)
+        sum_over_time("theta", 1, 2)
+        difference_and_tanh(0, 0, 1)
+        prepare_a(0, 5)
+        sum_over_time("theta", 1, 3)
+        high_half("theta", 1, FIRST)
+        low_half("theta", 1, FIRST)
+        difference_and_tanh(0, 0, 2)
+        difference_and_tanh(0, 0, 3)
+        take_out_th()
+        turn_halves(1, 0)
         for n in range(PIECES):
             difference_and_tanh(0, 1, n)
-        quantise_f(1, 0)
+        quantise_f(0, 0)
+        high_half("theta", 1, REST)
+        low_half("theta", 1, REST)
         quantise_f(0, 1)
+        difference_and_tanh(1, 0, 0)
+        difference_and_tanh(1, 0, 1)
+        difference_and_tanh(1, 0, 2)
+        difference_and_tanh(1, 0, 3)
+        for kt in range(6, K_TILES):
+            prepare_a(0, kt)
+        gpsimd_difference(2, 0)
+        for kt in range(K_TILES):
+            prepare_a(1, kt)
+        gpsimd_difference(2, 1)
+        for c in range(3, CHUNKS):
+            gpsimd_difference(c, 0)
+            gpsimd_difference(c, 1)
 
-        ahead = [(1, 1, n) for n in range(PIECES)]
+        ahead = [("pe", 1, 1, n) for n in range(PIECES)]
         for c in range(U_CHUNKS, CHUNKS):
-            ahead += [(c, g, n) for g in range(PASSES) for n in range(PIECES)]
-        to_turn = [(g, b) for b in range(1, B) for g in range(PASSES)]
-        to_quantise = {}
+            ahead += [("gpsimd", c, 0, 0), ("pe", c, 1, 0), ("pe", c, 1, 1), None,
+                      ("gpsimd", c, 0, 1), ("pe", c, 1, 2), ("pe", c, 1, 3), None]
+        to_quantise = {1: (1, 0)}
         for item in range(CHUNKS * K_TILES):
             multiply_and_store(*divmod(item, K_TILES))
-            if 0 <= item - 1 < len(to_turn):
-                turn_halves(*to_turn[item - 1])
-            if item < len(ahead):
-                c, g, n = ahead[item]
-                difference_and_tanh(c, g, n)
-                if n == PIECES - 1:
+            if item in (2, 3, 4):
+                turn_halves(1, item - 1)
+            if item < len(ahead) and ahead[item]:
+                engine, c, g, n = ahead[item]
+                if engine == "pe":
+                    difference_and_tanh(c, g, n)
+                else:
+                    gpsimd_tanh(c, n)
+                if n == (PIECES - 1 if engine == "pe" else 1):
                     to_quantise[item + QUANT_LAG] = (c, g)
             if item in to_quantise:
                 quantise_f(*to_quantise[item])

@@ -32,7 +32,7 @@ FLOPS = 2 * (B * T * V) * C * K * 2 + 2 * (B * V * V) * K * K
 
 
 def regroup_columns(copy, grouped_pool, rows):
-    grouped = grouped_pool.tile([P, N_TILE * PACK], BF16, name="grouped", align_bytes=64)
+    grouped = grouped_pool.tile([P, rows.shape[2] * PACK], BF16, name="grouped", align_bytes=64)
     copy(
         out=grouped[:].rearrange("p (c i s) -> p c s i", i=RUN, s=PACK),
         in_=rows.rearrange("p s (c i) -> p c s i", i=RUN),
@@ -65,6 +65,11 @@ def tile_attgcn_pa_kernel(
             )
         lam_bf = const.tile([P, 1], BF16, name="lam_bf")
         nc.scalar.dma_start(out=lam_bf[:], in_=lam.partition_broadcast(P))
+
+        warm = const.tile([P, 1], F32, name="warm")
+        nc.vector.memset(warm[:], 0.0)
+        warm_tanh = const.tile([P, 1], F32, name="warm_tanh")
+        nc.scalar.activation(out=warm_tanh[:], in_=warm[:], func=ACT.Tanh)
 
         def raw_tile(name):
             return raw_pool.tile([P, PACK * K], BF16, name=name, tag="raw")
@@ -138,8 +143,8 @@ def tile_attgcn_pa_kernel(
                         nc.tensor.transpose(
                             x_t[:, i, h, :], x_words[:, first : first + P], ident[:]
                         )
-                copy = nc.vector.tensor_copy if th == 0 else nc.scalar.copy
                 for i in range(2):
+                    copy = nc.vector.tensor_copy if (th, pair) == (0, 1) else nc.scalar.copy
                     copy(
                         out=x_grouped_words[:, th * T // 2 : (th + 1) * T // 2, 2 * pair + i, :, :],
                         in_=x_t[:, i, :, :].rearrange("q h (t v) -> q t v h", v=V),
@@ -155,7 +160,6 @@ def tile_attgcn_pa_kernel(
         turn_x(0)
         turn_x(1)
         nc.vector.tensor_copy(out=bias_rows_f32[:], in_=bias_rows[:])
-        quantise_x(0)
         bias_ps = psum_diff.tile([P, N_TILE], F32, name="bias_ps", tag="diff")
         nc.tensor.transpose(bias_ps[:, 0:P], bias_rows_f32[:], ident[:])
 
@@ -169,44 +173,46 @@ def tile_attgcn_pa_kernel(
 
         w_grouped = {}
 
-        def regroup_weights(name, g):
-            cols = slice(g * N_TILE, (g + 1) * N_TILE)
-            w_grouped[(name, g)] = regroup_columns(
-                w_copy[name], grouped_pool, w_rows[name][:, :, cols]
+        def regroup_weights(name, first, width=N_TILE):
+            w_grouped[(name, first)] = regroup_columns(
+                w_copy[name], grouped_pool, w_rows[name][:, :, first : first + width]
             )
 
-        def quantise_weights(name, g):
-            cols = slice(g * N_TILE, (g + 1) * N_TILE)
+        def quantise_weights(name, first, width=N_TILE):
+            cols = slice(first, first + width)
             nc.vector.quantize_mx(
                 out=w_codes[name][:, cols].bitcast(FP8X4), scales=w_scales[name][:, cols],
-                in_=w_grouped[(name, g)][:],
+                in_=w_grouped[(name, first)][:],
             )
 
-        regroup_weights("phi", 0)
-        regroup_weights("theta", 0)
-        quantise_x(1)
-        quantise_weights("phi", 0)
-
-        regroup_weights("phi", 1)
-        quantise_weights("theta", 0)
-        regroup_weights("theta", 1)
-
         bias_cols = const.tile([P, 3 * K_TILES], F32, name="bias_cols")
-        nc.vector.tensor_copy(out=bias_cols[:], in_=bias_ps[:, 0 : 3 * K_TILES])
+        nc.scalar.copy(out=bias_cols[:], in_=bias_ps[:, 0 : 3 * K_TILES])
         phi_b_cols = bias_cols[:, 0:K_TILES]
         theta_b_cols = bias_cols[:, K_TILES : 2 * K_TILES]
         kappa_b_cols = bias_cols[:, 2 * K_TILES : 3 * K_TILES]
         bias_diff = const.tile([P, K_TILES], F32, name="bias_diff")
-        nc.vector.tensor_sub(out=bias_diff[:], in0=phi_b_cols, in1=theta_b_cols)
+        nc.gpsimd.tensor_sub(out=bias_diff[:], in0=phi_b_cols, in1=theta_b_cols)
         lam_col = const.tile([P, 1], F32, name="lam_col")
-        nc.vector.tensor_copy(out=lam_col[:], in_=lam_bf[:])
+        nc.gpsimd.tensor_copy(out=lam_col[:], in_=lam_bf[:])
         bias_diff_t = const.tile([P, K_TILES], F32, name="bias_diff_t")
-        nc.vector.tensor_scalar_mul(out=bias_diff_t[:], in0=bias_diff[:], scalar1=float(T))
+        nc.gpsimd.tensor_scalar_mul(out=bias_diff_t[:], in0=bias_diff[:], scalar1=float(T))
         lam_kappa_b = const.tile([P, K_TILES], F32, name="lam_kappa_b")
-        nc.vector.tensor_scalar_mul(out=lam_kappa_b[:], in0=kappa_b_cols, scalar1=lam_col[:, 0:1])
+        nc.gpsimd.tensor_scalar_mul(out=lam_kappa_b[:], in0=kappa_b_cols, scalar1=lam_col[:, 0:1])
 
-        quantise_weights("phi", 1)
-        quantise_weights("theta", 1)
+        quantise_x(0)
+        regroup_weights("phi", 0, N_TILE // 2)
+        regroup_weights("theta", 0)
+        regroup_weights("phi", N_TILE // 2, N_TILE // 2)
+        quantise_x(1)
+        quantise_weights("phi", 0, N_TILE // 2)
+        quantise_weights("phi", N_TILE // 2, N_TILE // 2)
+
+        regroup_weights("phi", N_TILE)
+        quantise_weights("theta", 0)
+        regroup_weights("theta", N_TILE)
+
+        quantise_weights("phi", N_TILE)
+        quantise_weights("theta", N_TILE)
 
         a_plus = const.tile([P, U_CHUNKS, K_TILES, N_TILE], F32, name="a_plus")
 
@@ -416,55 +422,52 @@ def tile_attgcn_pa_kernel(
                 sum_over_time(name, g, j)
         open_sums("theta", 1)
         sum_over_time("theta", 1, 0)
+        prepare_a(0, 0)
         regroup_kappa(0, 0)
         add_bias(0, FIRST)
         high_half("phi", 0, FIRST)
         take_out_p()
         low_half("phi", 0, FIRST)
-        for kt in range(3):
+        for kt in range(1, 3):
             prepare_a(0, kt)
         regroup_kappa(1, 0)
         high_half("theta", 0, FIRST)
         low_half("theta", 0, FIRST)
+        for kt in range(3, 7):
+            prepare_a(0, kt)
         turn_halves(0, 0)
         quantise_kappa(0, 0)
-        quantise_kappa(1, 0)
-        for kt in range(3, 5):
-            prepare_a(0, kt)
-        regroup_kappa(0, 1)
         add_bias(1, ALL)
         high_half("phi", 1, ALL)
-        regroup_kappa(1, 1)
+        quantise_kappa(1, 0)
+        take_out_th()
         low_half("phi", 1, ALL)
-        quantise_kappa(0, 1)
-        quantise_kappa(1, 1)
         sum_over_time("theta", 1, 1)
         difference_and_tanh(0, 0, 0)
+        regroup_kappa(0, 1)
         sum_over_time("theta", 1, 2)
         difference_and_tanh(0, 0, 1)
-        prepare_a(0, 5)
         sum_over_time("theta", 1, 3)
         high_half("theta", 1, FIRST)
         low_half("theta", 1, FIRST)
         difference_and_tanh(0, 0, 2)
         difference_and_tanh(0, 0, 3)
-        take_out_th()
         turn_halves(1, 0)
+        regroup_kappa(1, 1)
+        quantise_f(0, 0)
         for n in range(PIECES):
             difference_and_tanh(0, 1, n)
-        quantise_f(0, 0)
+        quantise_kappa(0, 1)
+        quantise_kappa(1, 1)
         high_half("theta", 1, REST)
-        low_half("theta", 1, REST)
         quantise_f(0, 1)
-        difference_and_tanh(1, 0, 0)
-        difference_and_tanh(1, 0, 1)
-        difference_and_tanh(1, 0, 2)
-        difference_and_tanh(1, 0, 3)
-        for kt in range(6, K_TILES):
-            prepare_a(0, kt)
-        gpsimd_difference(2, 0)
-        for kt in range(K_TILES):
+        low_half("theta", 1, REST)
+        prepare_a(0, 7)
+        for n in range(PIECES):
+            difference_and_tanh(1, 0, n)
+        for kt in range(0, 8):
             prepare_a(1, kt)
+        gpsimd_difference(2, 0)
         gpsimd_difference(2, 1)
         for c in range(3, CHUNKS):
             gpsimd_difference(c, 0)
@@ -477,8 +480,8 @@ def tile_attgcn_pa_kernel(
         to_quantise = {1: (1, 0)}
         for item in range(CHUNKS * K_TILES):
             multiply_and_store(*divmod(item, K_TILES))
-            if item in (2, 3, 4):
-                turn_halves(1, item - 1)
+            if item in (2, 4, 6):
+                turn_halves(1, item // 2)
             if item < len(ahead) and ahead[item]:
                 engine, c, g, n = ahead[item]
                 if engine == "pe":

@@ -26,6 +26,7 @@ PIECES = N_TILE // P
 KINDS = 4
 RUN = 4
 U_GPSIMD = 4
+B_TENSOR = 2
 QUANT_LAG = 1
 
 FLOPS = 2 * (B * T * V) * C * K * 2 + 2 * (B * V * V) * K * K
@@ -250,7 +251,7 @@ def tile_attgcn_pa_kernel(
 
         halves = [
             const.tile([P, PACK, b_count, KINDS, V], BF16, name="halves", tag="halves%d" % b_count)
-            for b_count in (1, B)
+            for b_count in (B_TENSOR, B)
         ]
         p_biased = const.tile([P, PASSES, PACK, ROWS], F32, name="p_biased")
 
@@ -303,15 +304,15 @@ def tile_attgcn_pa_kernel(
 
         def take_out_p():
             nc.vector.tensor_tensor(
-                out=p_t[:, V:, :],
-                in0=sums[("phi", 0)][:, :, V:].rearrange("q j r -> q r j"),
-                in1=bias_diff_t[:, 0:PACK].unsqueeze(1).to_broadcast([P, ROWS - V, PACK]),
+                out=p_t[:, B_TENSOR * V :, :],
+                in0=sums[("phi", 0)][:, :, B_TENSOR * V :].rearrange("q j r -> q r j"),
+                in1=bias_diff_t[:, 0:PACK].unsqueeze(1).to_broadcast([P, ROWS - B_TENSOR * V, PACK]),
                 op=ALU.add,
             )
 
         def take_out_th():
             nc.vector.tensor_copy(
-                out=th_t[:, V:, :], in_=sums[("theta", 0)][:, :, V:].rearrange("q j r -> q r j")
+                out=th_t[:, B_TENSOR * V :, :], in_=sums[("theta", 0)][:, :, B_TENSOR * V :].rearrange("q j r -> q r j")
             )
 
         def gpsimd_difference(c, half):
@@ -414,6 +415,7 @@ def tile_attgcn_pa_kernel(
             nc.sync.dma_start(out=out_view[:, kt, cols], in_=result[:])
 
         FIRST = slice(0, 1)
+        TENSOR = slice(0, B_TENSOR)
         REST = slice(1, B)
         ALL = slice(0, B)
         for name, g in (("phi", 0), ("theta", 0), ("phi", 1)):
@@ -424,15 +426,15 @@ def tile_attgcn_pa_kernel(
         sum_over_time("theta", 1, 0)
         prepare_a(0, 0)
         regroup_kappa(0, 0)
-        add_bias(0, FIRST)
-        high_half("phi", 0, FIRST)
+        add_bias(0, TENSOR)
+        high_half("phi", 0, TENSOR)
         take_out_p()
-        low_half("phi", 0, FIRST)
+        low_half("phi", 0, TENSOR)
         for kt in range(1, 3):
             prepare_a(0, kt)
         regroup_kappa(1, 0)
-        high_half("theta", 0, FIRST)
-        low_half("theta", 0, FIRST)
+        high_half("theta", 0, TENSOR)
+        low_half("theta", 0, TENSOR)
         for kt in range(3, 7):
             prepare_a(0, kt)
         turn_halves(0, 0)
@@ -467,21 +469,23 @@ def tile_attgcn_pa_kernel(
             difference_and_tanh(1, 0, n)
         for kt in range(0, 8):
             prepare_a(1, kt)
-        gpsimd_difference(2, 0)
-        gpsimd_difference(2, 1)
-        for c in range(3, CHUNKS):
+        for c in range(B_TENSOR * U_CHUNKS, CHUNKS):
             gpsimd_difference(c, 0)
             gpsimd_difference(c, 1)
 
         ahead = [("pe", 1, 1, n) for n in range(PIECES)]
         for c in range(U_CHUNKS, CHUNKS):
-            ahead += [("gpsimd", c, 0, 0), ("pe", c, 1, 0), ("pe", c, 1, 1), None,
-                      ("gpsimd", c, 0, 1), ("pe", c, 1, 2), ("pe", c, 1, 3), None]
+            if c < B_TENSOR * U_CHUNKS:
+                ahead += [("pe", c, g, n) for g in range(PASSES) for n in range(PIECES)]
+            else:
+                ahead += [("gpsimd", c, 0, 0), ("pe", c, 1, 0), ("pe", c, 1, 1), None,
+                          ("gpsimd", c, 0, 1), ("pe", c, 1, 2), ("pe", c, 1, 3), None]
+        to_turn = {2: (0, 1), 4: (1, 1), 12: (1, 2), 20: (1, 3)}
         to_quantise = {1: (1, 0)}
         for item in range(CHUNKS * K_TILES):
             multiply_and_store(*divmod(item, K_TILES))
-            if item in (2, 4, 6):
-                turn_halves(1, item // 2)
+            if item in to_turn:
+                turn_halves(*to_turn[item])
             if item < len(ahead) and ahead[item]:
                 engine, c, g, n = ahead[item]
                 if engine == "pe":

@@ -27,18 +27,17 @@ KINDS = 4
 RUN = 4
 U_GPSIMD = 4
 B_TENSOR = 2
+STARTED = 3
 QUANT_LAG = 1
 
 FLOPS = 2 * (B * T * V) * C * K * 2 + 2 * (B * V * V) * K * K
 
 
-def regroup_columns(copy, grouped_pool, rows):
-    grouped = grouped_pool.tile([P, rows.shape[2] * PACK], BF16, name="grouped", align_bytes=64)
+def regroup_columns(copy, grouped, rows):
     copy(
-        out=grouped[:].rearrange("p (c i s) -> p c s i", i=RUN, s=PACK),
+        out=grouped.rearrange("p (c i s) -> p c s i", i=RUN, s=PACK),
         in_=rows.rearrange("p s (c i) -> p c s i", i=RUN),
     )
-    return grouped
 
 
 def tile_attgcn_pa_kernel(
@@ -48,12 +47,14 @@ def tile_attgcn_pa_kernel(
     with ExitStack() as stack:
         const = stack.enter_context(tc.tile_pool(name="const", bufs=1))
         raw_pool = stack.enter_context(tc.tile_pool(name="raw", bufs=7))
-        grouped_pool = stack.enter_context(tc.tile_pool(name="grouped", bufs=4))
+        grouped_pool = stack.enter_context(tc.tile_pool(name="grouped", bufs=5))
         f_pool = stack.enter_context(tc.tile_pool(name="f", bufs=5))
         diff_pool = stack.enter_context(tc.tile_pool(name="diff", bufs=4))
+        vector_diff_pool = stack.enter_context(tc.tile_pool(name="vector_diff", bufs=3))
         f_mx_pool = stack.enter_context(tc.tile_pool(name="f_mx", bufs=6))
         result_pool = stack.enter_context(tc.tile_pool(name="result", bufs=8))
-        psum_diff = stack.enter_context(tc.psum_pool(name="psum_diff", bufs=4))
+        psum_keep = stack.enter_context(tc.psum_pool(name="psum_keep", bufs=1))
+        psum_diff = stack.enter_context(tc.psum_pool(name="psum_diff", bufs=3))
         psum_acc = stack.enter_context(tc.psum_pool(name="psum_acc", bufs=4))
         stack.enter_context(tc.manual_schedule())
 
@@ -175,15 +176,17 @@ def tile_attgcn_pa_kernel(
         w_grouped = {}
 
         def regroup_weights(name, first, width=N_TILE):
-            w_grouped[(name, first)] = regroup_columns(
-                w_copy[name], grouped_pool, w_rows[name][:, :, first : first + width]
-            )
+            grouped = grouped_pool.tile(
+                [P, N_TILE * PACK], BF16, name="w_grouped", tag="grouped", align_bytes=64
+            )[:, 0 : width * PACK]
+            regroup_columns(w_copy[name], grouped, w_rows[name][:, :, first : first + width])
+            w_grouped[(name, first)] = grouped
 
         def quantise_weights(name, first, width=N_TILE):
             cols = slice(first, first + width)
             nc.vector.quantize_mx(
                 out=w_codes[name][:, cols].bitcast(FP8X4), scales=w_scales[name][:, cols],
-                in_=w_grouped[(name, first)][:],
+                in_=w_grouped[(name, first)],
             )
 
         bias_cols = const.tile([P, 3 * K_TILES], F32, name="bias_cols")
@@ -218,22 +221,17 @@ def tile_attgcn_pa_kernel(
         a_plus = const.tile([P, U_CHUNKS, K_TILES, N_TILE], F32, name="a_plus")
 
         def prepare_a(uc, kt):
-            if uc == 0:
-                nc.scalar.activation(
-                    out=a_plus[:, uc, kt, :], in_=a_raw[uc][:, kt, :], func=ACT.Identity,
-                    bias=lam_kappa_b[:, kt : kt + 1],
-                )
-            else:
-                nc.gpsimd.tensor_scalar(
-                    out=a_plus[:, uc, kt, :], in0=a_raw[uc][:, kt, :],
-                    scalar1=1.0, scalar2=lam_kappa_b[:, kt : kt + 1],
-                    op0=ALU.mult, op1=ALU.add,
-                )
+            nc.gpsimd.tensor_scalar(
+                out=a_plus[:, uc, kt, :], in0=a_raw[uc][:, kt, :],
+                scalar1=1.0, scalar2=lam_kappa_b[:, kt : kt + 1],
+                op0=ALU.mult, op1=ALU.add,
+            )
 
         sums = {}
 
         def open_sums(name, g):
-            sums[(name, g)] = psum_acc.tile([P, PACK, ROWS], F32, name="sum", tag="acc")
+            pool, tag = (psum_keep, "keep") if (name, g) == ("theta", 0) else (psum_acc, "acc")
+            sums[(name, g)] = pool.tile([P, PACK, ROWS], F32, name="sum", tag=tag)
 
         def sum_over_time(name, g, j):
             tile_cols = slice((g * PACK + j) * P, (g * PACK + j + 1) * P)
@@ -303,11 +301,9 @@ def tile_attgcn_pa_kernel(
         gpsimd_diff = {}
 
         def take_out_p():
-            nc.vector.tensor_tensor(
+            nc.vector.tensor_copy(
                 out=p_t[:, B_TENSOR * V :, :],
-                in0=sums[("phi", 0)][:, :, B_TENSOR * V :].rearrange("q j r -> q r j"),
-                in1=bias_diff_t[:, 0:PACK].unsqueeze(1).to_broadcast([P, ROWS - B_TENSOR * V, PACK]),
-                op=ALU.add,
+                in_=p_biased[:, 0, :, B_TENSOR * V :].rearrange("q j r -> q r j"),
             )
 
         def take_out_th():
@@ -340,6 +336,23 @@ def tile_attgcn_pa_kernel(
                 func=ACT.Tanh, scale=1.0 / T,
             )
 
+        vector_diff = {}
+
+        def vector_difference(c, g, n):
+            b, uc = divmod(c, U_CHUNKS)
+            rows = U_CHUNK // PIECES
+            first_u = b * V + uc * U_CHUNK + n * rows
+            diff = vector_diff_pool.tile([P, PACK, rows, V], F32, name="vector_diff")
+            nc.vector.tensor_tensor(
+                out=diff[:],
+                in0=p_biased[:, g, :, first_u : first_u + rows]
+                .unsqueeze(3).to_broadcast([P, PACK, rows, V]),
+                in1=sums[("theta", g)][:, :, b * V : (b + 1) * V]
+                .unsqueeze(2).to_broadcast([P, PACK, rows, V]),
+                op=ALU.subtract,
+            )
+            vector_diff[(c, g, n)] = diff
+
         f_bf16 = {}
         f_codes = {}
         f_scales = {}
@@ -348,21 +361,25 @@ def tile_attgcn_pa_kernel(
             b, uc = divmod(c, U_CHUNKS)
             if n == 0:
                 f_bf16[(c, g)] = f_pool.tile([P, N_TILE * PACK], BF16, name="f", align_bytes=64)
-            first = (uc * PIECES + n) * P
-            bank = psum_diff.tile([P, PACK, P], F32, name="diff_ps", tag="diff")
-            for j in range(PACK):
-                nc.tensor.matmul(
-                    bank[:, j, :],
-                    lhsT=turned[(g, b)][:, j * P : (j + 1) * P],
-                    rhs=choose_cols[:, first : first + P],
-                    start=True,
-                    stop=True,
-                )
+            if (c, g, n) in vector_diff:
+                difference = vector_diff[(c, g, n)][:].rearrange("q j u v -> q j (u v)")
+            else:
+                first = (uc * PIECES + n) * P
+                bank = psum_diff.tile([P, PACK, P], F32, name="diff_ps", tag="diff")
+                for j in range(PACK):
+                    nc.tensor.matmul(
+                        bank[:, j, :],
+                        lhsT=turned[(g, b)][:, j * P : (j + 1) * P],
+                        rhs=choose_cols[:, first : first + P],
+                        start=True,
+                        stop=True,
+                    )
+                difference = bank[:]
             nc.scalar.activation(
                 out=f_bf16[(c, g)][:, n * N_TILE : (n + 1) * N_TILE].rearrange(
                     "q (m j) -> q m j", j=PACK
                 ),
-                in_=bank[:].rearrange("q j m -> q m j"),
+                in_=difference.rearrange("q j m -> q m j"),
                 func=ACT.Tanh, scale=1.0 / T,
             )
 
@@ -379,9 +396,16 @@ def tile_attgcn_pa_kernel(
         kappa_scales = const.tile([P, PASSES, K], U8, name="kappa_scales", align_bytes=64)
         kappa_grouped = {}
 
-        def regroup_kappa(g, half):
-            kappa_grouped[(g, half)] = regroup_columns(
-                nc.vector.tensor_copy, grouped_pool, kappa_raw[half][:, g * PACK : (g + 1) * PACK, :]
+        def regroup_kappa(copy, g, half, part, parts):
+            if part == 0:
+                kappa_grouped[(g, half)] = grouped_pool.tile(
+                    [P, N_TILE * PACK], BF16, name="kappa_grouped", tag="grouped", align_bytes=64
+                )
+            width = N_TILE // parts
+            regroup_columns(
+                copy,
+                kappa_grouped[(g, half)][:, part * width * PACK : (part + 1) * width * PACK],
+                kappa_raw[half][:, g * PACK : (g + 1) * PACK, part * width : (part + 1) * width],
             )
 
         def quantise_kappa(g, half):
@@ -391,24 +415,28 @@ def tile_attgcn_pa_kernel(
                 in_=kappa_grouped[(g, half)][:],
             )
 
-        def multiply_and_store(c, kt):
+        acc = {}
+
+        def multiply(c, kt, g):
+            if g == 0:
+                acc[(c, kt)] = psum_acc.tile([P, N_TILE], F32, name="acc", tag="acc")
+            tile_cols = slice(kt * P, (kt + 1) * P)
+            nc.tensor.matmul_mx(
+                out=acc[(c, kt)][:],
+                lhsT=kappa_codes[:, g, tile_cols].bitcast(FP8X4),
+                lhsT_scale=kappa_scales[:, g, tile_cols],
+                rhs=f_codes[(c, g)][:].bitcast(FP8X4),
+                rhs_scale=f_scales[(c, g)][:],
+                start=(g == 0),
+                stop=(g == PASSES - 1),
+            )
+
+        def finish_and_store(c, kt):
             b, uc = divmod(c, U_CHUNKS)
             cols = slice(uc * N_TILE, (uc + 1) * N_TILE)
-            tile_cols = slice(kt * P, (kt + 1) * P)
-            acc = psum_acc.tile([P, N_TILE], F32, name="acc", tag="acc")
-            for g in range(PASSES):
-                nc.tensor.matmul_mx(
-                    out=acc[:],
-                    lhsT=kappa_codes[:, g, tile_cols].bitcast(FP8X4),
-                    lhsT_scale=kappa_scales[:, g, tile_cols],
-                    rhs=f_codes[(c, g)][:].bitcast(FP8X4),
-                    rhs_scale=f_scales[(c, g)][:],
-                    start=(g == 0),
-                    stop=(g == PASSES - 1),
-                )
             result = result_pool.tile([P, N_TILE], F32, name="result")
             nc.vector.scalar_tensor_tensor(
-                out=result[:], in0=acc[:], scalar=lam_col[:, 0:1], in1=a_plus[:, uc, kt, :],
+                out=result[:], in0=acc[(c, kt)][:], scalar=lam_col[:, 0:1], in1=a_plus[:, uc, kt, :],
                 op0=ALU.mult, op1=ALU.add,
             )
             out_view = out[b].rearrange("(a q) u v -> q a (u v)", q=P)
@@ -418,81 +446,93 @@ def tile_attgcn_pa_kernel(
         TENSOR = slice(0, B_TENSOR)
         REST = slice(1, B)
         ALL = slice(0, B)
-        for name, g in (("phi", 0), ("theta", 0), ("phi", 1)):
+        on_scalar, on_vector = nc.scalar.copy, nc.vector.tensor_copy
+        for name, g in (("phi", 0), ("theta", 0)):
             open_sums(name, g)
             for j in range(PACK):
                 sum_over_time(name, g, j)
-        open_sums("theta", 1)
-        sum_over_time("theta", 1, 0)
-        prepare_a(0, 0)
-        regroup_kappa(0, 0)
-        add_bias(0, TENSOR)
-        high_half("phi", 0, TENSOR)
-        take_out_p()
-        low_half("phi", 0, TENSOR)
-        for kt in range(1, 3):
+        open_sums("phi", 1)
+        for j in range(3):
+            sum_over_time("phi", 1, j)
+        for kt in range(K_TILES):
             prepare_a(0, kt)
-        regroup_kappa(1, 0)
+        regroup_kappa(on_scalar, 0, 0, 0, 2)
+        add_bias(0, ALL)
+        high_half("phi", 0, TENSOR)
+        low_half("phi", 0, TENSOR)
+        regroup_kappa(on_scalar, 0, 0, 1, 2)
         high_half("theta", 0, TENSOR)
         low_half("theta", 0, TENSOR)
-        for kt in range(3, 7):
-            prepare_a(0, kt)
         turn_halves(0, 0)
+        regroup_kappa(on_scalar, 1, 0, 0, 2)
+        take_out_th()
         quantise_kappa(0, 0)
+        regroup_kappa(on_vector, 1, 0, 1, 2)
+        sum_over_time("phi", 1, 3)
         add_bias(1, ALL)
         high_half("phi", 1, ALL)
         quantise_kappa(1, 0)
-        take_out_th()
         low_half("phi", 1, ALL)
-        sum_over_time("theta", 1, 1)
-        difference_and_tanh(0, 0, 0)
-        regroup_kappa(0, 1)
-        sum_over_time("theta", 1, 2)
-        difference_and_tanh(0, 0, 1)
-        sum_over_time("theta", 1, 3)
+        open_sums("theta", 1)
+        for j in range(PACK):
+            sum_over_time("theta", 1, j)
+            if j < 2:
+                difference_and_tanh(0, 0, j)
         high_half("theta", 1, FIRST)
         low_half("theta", 1, FIRST)
-        difference_and_tanh(0, 0, 2)
-        difference_and_tanh(0, 0, 3)
+        vector_difference(0, 1, 0)
+        vector_difference(0, 1, 1)
+        for n in range(2, PIECES):
+            difference_and_tanh(0, 0, n)
         turn_halves(1, 0)
-        regroup_kappa(1, 1)
         quantise_f(0, 0)
+        regroup_kappa(on_vector, 0, 1, 0, 1)
         for n in range(PIECES):
             difference_and_tanh(0, 1, n)
+        for kt in range(STARTED):
+            multiply(0, kt, 0)
         quantise_kappa(0, 1)
-        quantise_kappa(1, 1)
         high_half("theta", 1, REST)
         quantise_f(0, 1)
+        regroup_kappa(on_vector, 1, 1, 0, 1)
+        quantise_kappa(1, 1)
+        take_out_p()
         low_half("theta", 1, REST)
-        prepare_a(0, 7)
-        for n in range(PIECES):
+        for n in range(4):
             difference_and_tanh(1, 0, n)
-        for kt in range(0, 8):
-            prepare_a(1, kt)
         for c in range(B_TENSOR * U_CHUNKS, CHUNKS):
             gpsimd_difference(c, 0)
+            if c == B_TENSOR * U_CHUNKS:
+                for kt in range(K_TILES):
+                    prepare_a(1, kt)
             gpsimd_difference(c, 1)
 
-        ahead = [("pe", 1, 1, n) for n in range(PIECES)]
+        ahead = [[("pe", 1, 1, 0), ("pe", 1, 1, 1)], [("pe", 1, 1, 2)], [("pe", 1, 1, 3)]]
         for c in range(U_CHUNKS, CHUNKS):
             if c < B_TENSOR * U_CHUNKS:
-                ahead += [("pe", c, g, n) for g in range(PASSES) for n in range(PIECES)]
+                ahead += [[("pe", c, g, n)] for g in range(PASSES) for n in range(PIECES)]
             else:
-                ahead += [("gpsimd", c, 0, 0), ("pe", c, 1, 0), ("pe", c, 1, 1), None,
-                          ("gpsimd", c, 0, 1), ("pe", c, 1, 2), ("pe", c, 1, 3), None]
+                ahead += [[("gpsimd", c, 0, 0)], [("pe", c, 1, 0)], [("pe", c, 1, 1)], [],
+                          [("gpsimd", c, 0, 1)], [("pe", c, 1, 2)], [("pe", c, 1, 3)], []]
         to_turn = {2: (0, 1), 4: (1, 1), 12: (1, 2), 20: (1, 3)}
+        vector_pieces = {4: (2, 0, 3), 9: (3, 0, 3)}
         to_quantise = {1: (1, 0)}
         for item in range(CHUNKS * K_TILES):
-            multiply_and_store(*divmod(item, K_TILES))
+            c, kt = divmod(item, K_TILES)
+            if item >= STARTED:
+                multiply(c, kt, 0)
+            multiply(c, kt, 1)
+            finish_and_store(c, kt)
             if item in to_turn:
                 turn_halves(*to_turn[item])
-            if item < len(ahead) and ahead[item]:
-                engine, c, g, n = ahead[item]
+            for engine, c, g, n in ahead[item] if item < len(ahead) else ():
                 if engine == "pe":
                     difference_and_tanh(c, g, n)
                 else:
                     gpsimd_tanh(c, n)
                 if n == (PIECES - 1 if engine == "pe" else 1):
                     to_quantise[item + QUANT_LAG] = (c, g)
+            if item in vector_pieces:
+                vector_difference(*vector_pieces[item])
             if item in to_quantise:
                 quantise_f(*to_quantise[item])

from contextlib import ExitStack

import concourse.mybir as mybir
from concourse.masks import make_identity

F32 = mybir.dt.float32
BF16 = mybir.dt.bfloat16
U32 = mybir.dt.uint32
U8 = mybir.dt.uint8
FP8X4 = mybir.dt.float8_e4m3fn_x4
ALU = mybir.AluOpType
ACT = mybir.ActivationFunctionType

P = 128
PACK = 4
B, T, V, C, K = 4, 8, 32, 512, 1024
ROWS = B * V
X_TILES = B * T * V // P
PASSES = K // (P * PACK)
K_TILES = K // P
N_TILE = 512
U_CHUNK = N_TILE // V
U_CHUNKS = V // U_CHUNK
CHUNKS = B * U_CHUNKS
PIECES = N_TILE // P
KINDS = 4
RUN = 4
U_GPSIMD = 4
B_TENSOR = 2
STARTED = 3
QUANT_LAG = 1

FLOPS = 2 * (B * T * V) * C * K * 2 + 2 * (B * V * V) * K * K


def regroup_columns(copy, grouped, rows):
    copy(
        out=grouped.rearrange("p (c i s) -> p c s i", i=RUN, s=PACK),
        in_=rows.rearrange("p s (c i) -> p c s i", i=RUN),
    )


def tile_attgcn_pa_kernel(
    tc, x, A, lam, phi_w, phi_b, theta_w, theta_b, kappa_w, kappa_b, out
):
    nc = tc.nc
    with ExitStack() as stack:
        const = stack.enter_context(tc.tile_pool(name="const", bufs=1))
        raw_pool = stack.enter_context(tc.tile_pool(name="raw", bufs=7))
        grouped_pool = stack.enter_context(tc.tile_pool(name="grouped", bufs=5))
        f_pool = stack.enter_context(tc.tile_pool(name="f", bufs=5))
        diff_pool = stack.enter_context(tc.tile_pool(name="diff", bufs=4))
        vector_diff_pool = stack.enter_context(tc.tile_pool(name="vector_diff", bufs=3))
        f_mx_pool = stack.enter_context(tc.tile_pool(name="f_mx", bufs=6))
        result_pool = stack.enter_context(tc.tile_pool(name="result", bufs=8))
        psum_keep = stack.enter_context(tc.psum_pool(name="psum_keep", bufs=1))
        psum_diff = stack.enter_context(tc.psum_pool(name="psum_diff", bufs=3))
        psum_acc = stack.enter_context(tc.psum_pool(name="psum_acc", bufs=4))
        stack.enter_context(tc.manual_schedule())

        bias_rows = const.tile([P, P], BF16, name="bias_rows")
        nc.vector.memset(bias_rows[:], 0.0)
        for i, bias in enumerate((phi_b, theta_b, kappa_b)):
            nc.scalar.dma_start(
                out=bias_rows[i * K_TILES : (i + 1) * K_TILES, :],
                in_=bias.rearrange("(r q) -> r q", q=P),
            )
        lam_bf = const.tile([P, 1], BF16, name="lam_bf")
        nc.scalar.dma_start(out=lam_bf[:], in_=lam.partition_broadcast(P))

        warm = const.tile([P, 1], F32, name="warm")
        nc.vector.memset(warm[:], 0.0)
        warm_tanh = const.tile([P, 1], F32, name="warm_tanh")
        nc.scalar.activation(out=warm_tanh[:], in_=warm[:], func=ACT.Tanh)

        def raw_tile(name):
            return raw_pool.tile([P, PACK * K], BF16, name=name, tag="raw")

        x_raw = raw_tile("x_raw")
        x_rows = x_raw[:].rearrange("p (n c) -> p n c", c=C)
        x_view = x.flatten_outer_dims().rearrange("(n p) c -> p n c", p=P)
        for th in range(2):
            nc.sync.dma_start(out=x_rows[:, th::2, :], in_=x_view[:, th::2, :])

        w_raw = {"phi": raw_tile("phi_raw"), "theta": raw_tile("theta_raw")}
        w_dram = {"phi": phi_w, "theta": theta_w}
        for g in range(PASSES):
            cols = slice(g * N_TILE, (g + 1) * N_TILE)
            for name in ("phi", "theta"):
                for h in range(2):
                    nc.sync.dma_start(
                        out=w_raw[name][:].rearrange("q (h e n) -> q h e n", h=2, e=2)[:, h, :, cols],
                        in_=w_dram[name].rearrange("(h q e) n -> q h e n", h=2, e=2)[:, h, :, cols],
                    )

        a_view = A.rearrange("(a q) u v -> q a (u v)", q=P)
        kappa_view = kappa_w.rearrange("(a q) n -> q a n", q=P)
        a_raw = []
        kappa_raw = []
        for raws, name, view, half in (
            (kappa_raw, "kappa_raw0", kappa_view, 0),
            (a_raw, "a_raw0", a_view, 0),
            (kappa_raw, "kappa_raw1", kappa_view, 1),
            (a_raw, "a_raw1", a_view, 1),
        ):
            raw = raw_tile(name)[:].rearrange("q (a n) -> q a n", n=N_TILE)
            nc.sync.dma_start(out=raw, in_=view[:, :, half * N_TILE : (half + 1) * N_TILE])
            raws.append(raw)

        ident = const.tile([P, P], F32, name="ident")
        make_identity(nc, ident[:])
        ident_bf = const.tile([P, P], BF16, name="ident_bf")
        nc.vector.tensor_copy(out=ident_bf[:], in_=ident[:])

        bias_rows_f32 = const.tile([P, P], F32, name="bias_rows_f32")

        is_u = const.tile([P, V], F32, name="is_u")
        nc.vector.tensor_add(out=is_u[:], in0=ident[:, 0:V], in1=ident[:, V : 2 * V])
        is_v = const.tile([P, V], F32, name="is_v")
        nc.vector.tensor_add(out=is_v[:], in0=ident[:, 2 * V : 3 * V], in1=ident[:, 3 * V : 4 * V])
        choose = const.tile([P, V, V], BF16, name="choose")
        nc.vector.tensor_tensor(
            out=choose[:],
            in0=is_u[:].unsqueeze(2).to_broadcast([P, V, V]),
            in1=is_v[:].unsqueeze(1).to_broadcast([P, V, V]),
            op=ALU.subtract,
        )
        choose_cols = choose[:].rearrange("p u v -> p (u v)")

        x_words = x_raw[:].bitcast(F32)
        x_grouped = const.tile([P, T * ROWS * PACK], BF16, name="x_grouped", align_bytes=64)
        x_grouped_words = x_grouped[:].bitcast(F32).rearrange(
            "q (t b v h) -> q t b v h", t=T, b=B, v=V
        )
        words = C // 2
        x_codes = const.tile([P, T * ROWS], U32, name="x_codes", align_bytes=64)
        x_scales = const.tile([P, T * ROWS], U8, name="x_scales", align_bytes=64)

        def turn_x(th):
            for pair in range(B // 2):
                x_t = psum_diff.tile([P, 2, 2, P], F32, name="x_t", tag="diff")
                for i in range(2):
                    for h in range(2):
                        first = (2 * (2 * pair + i) + th) * words + h * P
                        nc.tensor.transpose(
                            x_t[:, i, h, :], x_words[:, first : first + P], ident[:]
                        )
                for i in range(2):
                    copy = nc.vector.tensor_copy if (th, pair) == (0, 1) else nc.scalar.copy
                    copy(
                        out=x_grouped_words[:, th * T // 2 : (th + 1) * T // 2, 2 * pair + i, :, :],
                        in_=x_t[:, i, :, :].rearrange("q h (t v) -> q t v h", v=V),
                    )

        def quantise_x(th):
            cols = slice(th * T * ROWS // 2, (th + 1) * T * ROWS // 2)
            nc.vector.quantize_mx(
                out=x_codes[:, cols].bitcast(FP8X4), scales=x_scales[:, cols],
                in_=x_grouped[:, th * T * ROWS * PACK // 2 : (th + 1) * T * ROWS * PACK // 2],
            )

        turn_x(0)
        turn_x(1)
        nc.vector.tensor_copy(out=bias_rows_f32[:], in_=bias_rows[:])
        bias_ps = psum_diff.tile([P, N_TILE], F32, name="bias_ps", tag="diff")
        nc.tensor.transpose(bias_ps[:, 0:P], bias_rows_f32[:], ident[:])

        w_codes = {}
        w_scales = {}
        for name in ("phi", "theta"):
            w_codes[name] = const.tile([P, K], U32, name=name + "_codes", align_bytes=64)
            w_scales[name] = const.tile([P, K], U8, name=name + "_scales", align_bytes=64)
        w_rows = {name: w_raw[name][:].rearrange("q (s n) -> q s n", s=PACK) for name in w_raw}
        w_copy = {"phi": nc.vector.tensor_copy, "theta": nc.scalar.copy}

        w_grouped = {}

        def regroup_weights(name, first, width=N_TILE):
            grouped = grouped_pool.tile(
                [P, N_TILE * PACK], BF16, name="w_grouped", tag="grouped", align_bytes=64
            )[:, 0 : width * PACK]
            regroup_columns(w_copy[name], grouped, w_rows[name][:, :, first : first + width])
            w_grouped[(name, first)] = grouped

        def quantise_weights(name, first, width=N_TILE):
            cols = slice(first, first + width)
            nc.vector.quantize_mx(
                out=w_codes[name][:, cols].bitcast(FP8X4), scales=w_scales[name][:, cols],
                in_=w_grouped[(name, first)],
            )

        bias_cols = const.tile([P, 3 * K_TILES], F32, name="bias_cols")
        nc.scalar.copy(out=bias_cols[:], in_=bias_ps[:, 0 : 3 * K_TILES])
        phi_b_cols = bias_cols[:, 0:K_TILES]
        theta_b_cols = bias_cols[:, K_TILES : 2 * K_TILES]
        kappa_b_cols = bias_cols[:, 2 * K_TILES : 3 * K_TILES]
        bias_diff = const.tile([P, K_TILES], F32, name="bias_diff")
        nc.gpsimd.tensor_sub(out=bias_diff[:], in0=phi_b_cols, in1=theta_b_cols)
        lam_col = const.tile([P, 1], F32, name="lam_col")
        nc.gpsimd.tensor_copy(out=lam_col[:], in_=lam_bf[:])
        bias_diff_t = const.tile([P, K_TILES], F32, name="bias_diff_t")
        nc.gpsimd.tensor_scalar_mul(out=bias_diff_t[:], in0=bias_diff[:], scalar1=float(T))
        lam_kappa_b = const.tile([P, K_TILES], F32, name="lam_kappa_b")
        nc.gpsimd.tensor_scalar_mul(out=lam_kappa_b[:], in0=kappa_b_cols, scalar1=lam_col[:, 0:1])

        quantise_x(0)
        regroup_weights("phi", 0, N_TILE // 2)
        regroup_weights("theta", 0)
        regroup_weights("phi", N_TILE // 2, N_TILE // 2)
        quantise_x(1)
        quantise_weights("phi", 0, N_TILE // 2)
        quantise_weights("phi", N_TILE // 2, N_TILE // 2)

        regroup_weights("phi", N_TILE)
        quantise_weights("theta", 0)
        regroup_weights("theta", N_TILE)

        quantise_weights("phi", N_TILE)
        quantise_weights("theta", N_TILE)

        a_plus = const.tile([P, U_CHUNKS, K_TILES, N_TILE], F32, name="a_plus")

        def prepare_a(uc, kt):
            nc.gpsimd.tensor_scalar(
                out=a_plus[:, uc, kt, :], in0=a_raw[uc][:, kt, :],
                scalar1=1.0, scalar2=lam_kappa_b[:, kt : kt + 1],
                op0=ALU.mult, op1=ALU.add,
            )

        sums = {}

        def open_sums(name, g):
            pool, tag = (psum_keep, "keep") if (name, g) == ("theta", 0) else (psum_acc, "acc")
            sums[(name, g)] = pool.tile([P, PACK, ROWS], F32, name="sum", tag=tag)

        def sum_over_time(name, g, j):
            tile_cols = slice((g * PACK + j) * P, (g * PACK + j + 1) * P)
            for t in range(T):
                step_cols = slice(t * ROWS, (t + 1) * ROWS)
                nc.tensor.matmul_mx(
                    out=sums[(name, g)][:, j, :],
                    lhsT=w_codes[name][:, tile_cols].bitcast(FP8X4),
                    lhsT_scale=w_scales[name][:, tile_cols],
                    rhs=x_codes[:, step_cols].bitcast(FP8X4),
                    rhs_scale=x_scales[:, step_cols],
                    start=(t == 0),
                    stop=(t == T - 1),
                )

        halves = [
            const.tile([P, PACK, b_count, KINDS, V], BF16, name="halves", tag="halves%d" % b_count)
            for b_count in (B_TENSOR, B)
        ]
        p_biased = const.tile([P, PASSES, PACK, ROWS], F32, name="p_biased")

        def add_bias(g, batches):
            rows = slice(batches.start * V, batches.stop * V)
            width = (batches.stop - batches.start) * V
            nc.vector.tensor_tensor(
                out=p_biased[:, g, :, rows],
                in0=sums[("phi", g)][:, :, rows],
                in1=bias_diff_t[:, g * PACK : (g + 1) * PACK].unsqueeze(2).to_broadcast(
                    [P, PACK, width]
                ),
                op=ALU.add,
            )

        def whole(name, g, batches):
            tile = p_biased[:, g, :, :] if name == "phi" else sums[("theta", g)][:]
            return tile.rearrange("q j (b w) -> q j b w", b=B)[:, :, batches, :]

        def high_half(name, g, batches):
            kind = 0 if name == "phi" else 2
            nc.scalar.copy(out=halves[g][:, :, batches, kind, :], in_=whole(name, g, batches))

        def low_half(name, g, batches):
            kind = 0 if name == "phi" else 2
            nc.vector.tensor_tensor(
                out=halves[g][:, :, batches, kind + 1, :],
                in0=whole(name, g, batches),
                in1=halves[g][:, :, batches, kind, :],
                op=ALU.subtract,
            )

        turned = {}

        def turn_halves(g, b):
            bank = psum_diff.tile([P, 2 * N_TILE], BF16, name="turn_ps", tag="diff")
            for j in range(PACK):
                nc.tensor.transpose(
                    bank[:, j * P : (j + 1) * P],
                    halves[g][:, j, b, :, :].rearrange("q k w -> q (k w)"),
                    ident_bf[:],
                )
            tile = const.tile([P, N_TILE], BF16, name="turned_%d_%d" % (g, b), align_bytes=64)
            nc.scalar.copy(out=tile[:], in_=bank[:, 0:N_TILE])
            turned[(g, b)] = tile

        p_t = const.tile([P, ROWS, PACK], F32, name="p_t")
        th_t = const.tile([P, ROWS, PACK], F32, name="th_t")
        gpsimd_diff = {}

        def take_out_p():
            nc.vector.tensor_copy(
                out=p_t[:, B_TENSOR * V :, :],
                in_=p_biased[:, 0, :, B_TENSOR * V :].rearrange("q j r -> q r j"),
            )

        def take_out_th():
            nc.vector.tensor_copy(
                out=th_t[:, B_TENSOR * V :, :], in_=sums[("theta", 0)][:, :, B_TENSOR * V :].rearrange("q j r -> q r j")
            )

        def gpsimd_difference(c, half):
            b, uc = divmod(c, U_CHUNKS)
            diff = diff_pool.tile([P, U_CHUNK // 2, V, PACK], F32, name="diff")
            for i in range(0, U_CHUNK // 2, U_GPSIMD):
                first_u = b * V + uc * U_CHUNK + half * U_CHUNK // 2 + i
                nc.gpsimd.tensor_tensor(
                    out=diff[:, i : i + U_GPSIMD, :, :],
                    in0=p_t[:, first_u : first_u + U_GPSIMD, :]
                    .unsqueeze(2).to_broadcast([P, U_GPSIMD, V, PACK]),
                    in1=th_t[:, b * V : (b + 1) * V, :]
                    .unsqueeze(1).to_broadcast([P, U_GPSIMD, V, PACK]),
                    op=ALU.subtract,
                )
            gpsimd_diff[(c, half)] = diff

        def gpsimd_tanh(c, half):
            if half == 0:
                f_bf16[(c, 0)] = f_pool.tile([P, N_TILE * PACK], BF16, name="f", align_bytes=64)
            width = N_TILE * PACK // 2
            nc.scalar.activation(
                out=f_bf16[(c, 0)][:, half * width : (half + 1) * width],
                in_=gpsimd_diff[(c, half)][:].rearrange("q u v j -> q (u v j)"),
                func=ACT.Tanh, scale=1.0 / T,
            )

        vector_diff = {}

        def vector_difference(c, g, n):
            b, uc = divmod(c, U_CHUNKS)
            rows = U_CHUNK // PIECES
            first_u = b * V + uc * U_CHUNK + n * rows
            diff = vector_diff_pool.tile([P, PACK, rows, V], F32, name="vector_diff")
            nc.vector.tensor_tensor(
                out=diff[:],
                in0=p_biased[:, g, :, first_u : first_u + rows]
                .unsqueeze(3).to_broadcast([P, PACK, rows, V]),
                in1=sums[("theta", g)][:, :, b * V : (b + 1) * V]
                .unsqueeze(2).to_broadcast([P, PACK, rows, V]),
                op=ALU.subtract,
            )
            vector_diff[(c, g, n)] = diff

        f_bf16 = {}
        f_codes = {}
        f_scales = {}

        def difference_and_tanh(c, g, n):
            b, uc = divmod(c, U_CHUNKS)
            if n == 0:
                f_bf16[(c, g)] = f_pool.tile([P, N_TILE * PACK], BF16, name="f", align_bytes=64)
            if (c, g, n) in vector_diff:
                difference = vector_diff[(c, g, n)][:].rearrange("q j u v -> q j (u v)")
            else:
                first = (uc * PIECES + n) * P
                bank = psum_diff.tile([P, PACK, P], F32, name="diff_ps", tag="diff")
                for j in range(PACK):
                    nc.tensor.matmul(
                        bank[:, j, :],
                        lhsT=turned[(g, b)][:, j * P : (j + 1) * P],
                        rhs=choose_cols[:, first : first + P],
                        start=True,
                        stop=True,
                    )
                difference = bank[:]
            nc.scalar.activation(
                out=f_bf16[(c, g)][:, n * N_TILE : (n + 1) * N_TILE].rearrange(
                    "q (m j) -> q m j", j=PACK
                ),
                in_=difference.rearrange("q j m -> q m j"),
                func=ACT.Tanh, scale=1.0 / T,
            )

        def quantise_f(c, g):
            codes = f_mx_pool.tile([P, N_TILE], U32, name="f_codes", align_bytes=64)
            scales = f_mx_pool.tile([P, N_TILE], U8, name="f_scales", align_bytes=64)
            nc.vector.quantize_mx(
                out=codes[:].bitcast(FP8X4), scales=scales[:], in_=f_bf16[(c, g)][:]
            )
            f_codes[(c, g)] = codes
            f_scales[(c, g)] = scales

        kappa_codes = const.tile([P, PASSES, K], U32, name="kappa_codes", align_bytes=64)
        kappa_scales = const.tile([P, PASSES, K], U8, name="kappa_scales", align_bytes=64)
        kappa_grouped = {}

        def regroup_kappa(copy, g, half, part, parts):
            if part == 0:
                kappa_grouped[(g, half)] = grouped_pool.tile(
                    [P, N_TILE * PACK], BF16, name="kappa_grouped", tag="grouped", align_bytes=64
                )
            width = N_TILE // parts
            regroup_columns(
                copy,
                kappa_grouped[(g, half)][:, part * width * PACK : (part + 1) * width * PACK],
                kappa_raw[half][:, g * PACK : (g + 1) * PACK, part * width : (part + 1) * width],
            )

        def quantise_kappa(g, half):
            cols = slice(half * N_TILE, (half + 1) * N_TILE)
            nc.vector.quantize_mx(
                out=kappa_codes[:, g, cols].bitcast(FP8X4), scales=kappa_scales[:, g, cols],
                in_=kappa_grouped[(g, half)][:],
            )

        acc = {}

        def multiply(c, kt, g):
            if g == 0:
                acc[(c, kt)] = psum_acc.tile([P, N_TILE], F32, name="acc", tag="acc")
            tile_cols = slice(kt * P, (kt + 1) * P)
            nc.tensor.matmul_mx(
                out=acc[(c, kt)][:],
                lhsT=kappa_codes[:, g, tile_cols].bitcast(FP8X4),
                lhsT_scale=kappa_scales[:, g, tile_cols],
                rhs=f_codes[(c, g)][:].bitcast(FP8X4),
                rhs_scale=f_scales[(c, g)][:],
                start=(g == 0),
                stop=(g == PASSES - 1),
            )

        def finish_and_store(c, kt):
            b, uc = divmod(c, U_CHUNKS)
            cols = slice(uc * N_TILE, (uc + 1) * N_TILE)
            result = result_pool.tile([P, N_TILE], F32, name="result")
            nc.vector.scalar_tensor_tensor(
                out=result[:], in0=acc[(c, kt)][:], scalar=lam_col[:, 0:1], in1=a_plus[:, uc, kt, :],
                op0=ALU.mult, op1=ALU.add,
            )
            out_view = out[b].rearrange("(a q) u v -> q a (u v)", q=P)
            nc.sync.dma_start(out=out_view[:, kt, cols], in_=result[:])

        FIRST = slice(0, 1)
        TENSOR = slice(0, B_TENSOR)
        REST = slice(1, B)
        ALL = slice(0, B)
        on_scalar, on_vector = nc.scalar.copy, nc.vector.tensor_copy
        for name, g in (("phi", 0), ("theta", 0)):
            open_sums(name, g)
            for j in range(PACK):
                sum_over_time(name, g, j)
        open_sums("phi", 1)
        for j in range(3):
            sum_over_time("phi", 1, j)
        for kt in range(K_TILES):
            prepare_a(0, kt)
        regroup_kappa(on_scalar, 0, 0, 0, 2)
        add_bias(0, ALL)
        high_half("phi", 0, TENSOR)
        low_half("phi", 0, TENSOR)
        regroup_kappa(on_scalar, 0, 0, 1, 2)
        high_half("theta", 0, TENSOR)
        low_half("theta", 0, TENSOR)
        turn_halves(0, 0)
        regroup_kappa(on_scalar, 1, 0, 0, 2)
        take_out_th()
        quantise_kappa(0, 0)
        regroup_kappa(on_vector, 1, 0, 1, 2)
        sum_over_time("phi", 1, 3)
        add_bias(1, ALL)
        high_half("phi", 1, ALL)
        quantise_kappa(1, 0)
        low_half("phi", 1, ALL)
        open_sums("theta", 1)
        for j in range(PACK):
            sum_over_time("theta", 1, j)
            if j < 2:
                difference_and_tanh(0, 0, j)
        high_half("theta", 1, FIRST)
        low_half("theta", 1, FIRST)
        vector_difference(0, 1, 0)
        vector_difference(0, 1, 1)
        for n in range(2, PIECES):
            difference_and_tanh(0, 0, n)
        turn_halves(1, 0)
        quantise_f(0, 0)
        regroup_kappa(on_vector, 0, 1, 0, 1)
        for n in range(PIECES):
            difference_and_tanh(0, 1, n)
        for kt in range(STARTED):
            multiply(0, kt, 0)
        quantise_kappa(0, 1)
        high_half("theta", 1, REST)
        quantise_f(0, 1)
        regroup_kappa(on_vector, 1, 1, 0, 1)
        quantise_kappa(1, 1)
        take_out_p()
        low_half("theta", 1, REST)
        for n in range(4):
            difference_and_tanh(1, 0, n)
        for c in range(B_TENSOR * U_CHUNKS, CHUNKS):
            gpsimd_difference(c, 0)
            if c == B_TENSOR * U_CHUNKS:
                for kt in range(K_TILES):
                    prepare_a(1, kt)
            gpsimd_difference(c, 1)

        ahead = [[("pe", 1, 1, 0), ("pe", 1, 1, 1)], [("pe", 1, 1, 2)], [("pe", 1, 1, 3)]]
        for c in range(U_CHUNKS, CHUNKS):
            if c < B_TENSOR * U_CHUNKS:
                ahead += [[("pe", c, g, n)] for g in range(PASSES) for n in range(PIECES)]
            else:
                ahead += [[("gpsimd", c, 0, 0)], [("pe", c, 1, 0)], [("pe", c, 1, 1)], [],
                          [("gpsimd", c, 0, 1)], [("pe", c, 1, 2)], [("pe", c, 1, 3)], []]
        to_turn = {2: (0, 1), 4: (1, 1), 12: (1, 2), 20: (1, 3)}
        vector_pieces = {4: (2, 0, 3), 9: (3, 0, 3)}
        to_quantise = {1: (1, 0)}
        for item in range(CHUNKS * K_TILES):
            c, kt = divmod(item, K_TILES)
            if item >= STARTED:
                multiply(c, kt, 0)
            multiply(c, kt, 1)
            finish_and_store(c, kt)
            if item in to_turn:
                turn_halves(*to_turn[item])
            for engine, c, g, n in ahead[item] if item < len(ahead) else ():
                if engine == "pe":
                    difference_and_tanh(c, g, n)
                else:
                    gpsimd_tanh(c, n)
                if n == (PIECES - 1 if engine == "pe" else 1):
                    to_quantise[item + QUANT_LAG] = (c, g)
            if item in vector_pieces:
                vector_difference(*vector_pieces[item])
            if item in to_quantise:
                quantise_f(*to_quantise[item])
